import numpy as np
import ml_dtypes


def mxq(x, axis, fmt="e4m3"):
    dtype, down = {"e4m3": (ml_dtypes.float8_e4m3fn, 7), "e5m2": (ml_dtypes.float8_e5m2, 14)}[fmt]
    v = np.moveaxis(np.asarray(x, np.float32).astype(ml_dtypes.bfloat16).astype(np.float64), axis, -1)
    blocks = v.reshape(v.shape[:-1] + (-1, 32))
    amax = np.abs(blocks).max(-1, keepdims=True)
    byte = np.maximum(np.where(amax > 0, np.frexp(amax)[1] - 1 + 127, 0) - down, 1)
    scale = np.exp2(byte - 127.0)
    codes = (blocks / scale).astype(np.float32).astype(dtype).astype(np.float64)
    return np.moveaxis((codes * scale).reshape(v.shape), -1, axis)


WIDE = False


def mx_kscale(k):
    if not WIDE:
        return np.ones(k)
    levels = np.array([10, -10, 5, -5, 0])
    a = np.random.permutation(np.resize(levels, k // 512 * 4)).reshape(k // 512, 4)
    idx = np.arange(k)
    return np.exp2(a[idx // 512, idx % 128 // 32])


BF16 = ml_dtypes.bfloat16


def bf(x):
    return np.asarray(x, np.float32).astype(BF16)


def f64(x):
    return np.asarray(x).astype(np.float64)


B, I, M, O = 16384, 9, 2, 128
R = M ** I
NW = I // 2
EPS = 1e-6
C = 2.0 ** -14


def setup_inputs():
    x = np.random.standard_normal((B, I)) * np.sqrt(24.0 / I) * C
    means = np.random.standard_normal((I, M)) * 0.5 * C
    sign = np.where(np.random.standard_normal((I, M)) < 0.0, -1.0, 1.0)
    sigmas = sign * (0.85 + 0.3 * np.random.random((I, M))) * C
    rules = np.random.standard_normal((R, O)) * 4.0
    lv = np.unique(np.log2(mx_kscale(R)))
    e = lv[np.arange(NW * M) % len(lv)].reshape(NW, M)
    a = e.max(axis=1, keepdims=True) - e
    wide = len(lv) > 1
    sigmas[:NW] *= 32.0 if wide else 1.0
    means[:NW] += np.sqrt(2.0 * np.log(2.0) * a) * (np.abs(sigmas[:NW]) + EPS)
    A = np.zeros(1)
    for i in range(NW):
        A = (A[:, None] + a[i][None, :]).reshape(-1)
    rules = rules * np.exp2(np.repeat(A, R // len(A)))[:, None] / (np.sqrt(len(A)) if wide else 1.0)
    return {"x": bf(x), "mfs": bf(np.stack([means, sigmas], axis=2)), "rules": bf(rules)}


def reference(x, mfs, rules):
    x, mfs = f64(x), f64(mfs)
    means = mfs[:, :, 0]
    sigmas = np.abs(mfs[:, :, 1]) + EPS
    z = (x[:, :, None] - means[None]) / sigmas[None]
    memb = np.exp(-0.5 * z * z)
    nb = x.shape[0]
    strengths = np.ones((nb, 1))
    for i in range(I):
        strengths = (strengths[:, :, None] * memb[:, i, None, :]).reshape(nb, -1)
    norm = strengths / (np.sum(strengths, axis=1, keepdims=True) + EPS)
    return mxq(norm, 1, "e4m3") @ mxq(f64(rules), 0, "e4m3")

@@ -1,0 +1,246 @@
+from contextlib import ExitStack
+
+import concourse.mybir as mybir
+from concourse.masks import make_identity
+
+F32 = mybir.dt.float32
+BF16 = mybir.dt.bfloat16
+U32 = mybir.dt.uint32
+U8 = mybir.dt.uint8
+FP8X4 = mybir.dt.float8_e4m3fn_x4
+ALU = mybir.AluOpType
+ACT = mybir.ActivationFunctionType
+
+P = 128
+B, I, M, O = 16384, 9, 2, 128
+R = 512
+NJ = B // P
+EPS = 1e-6
+FLOPS = 2 * B * R * O
+CHUNKS = [4, 12] + [16] * 7
+QUAD = 4
+NQ = NJ // QUAD
+GROUP = 4
+LAG = 2
+
+
+def tile_extendedanfis_t_kernel(tc, x, mfs, rules, out):
+    nc = tc.nc
+    with ExitStack() as ctx:
+        const = ctx.enter_context(tc.tile_pool(name="const", bufs=1))
+        small = ctx.enter_context(tc.tile_pool(name="small", bufs=2))
+        s7p = ctx.enter_context(tc.tile_pool(name="s7p", bufs=2))
+        nbp = ctx.enter_context(tc.tile_pool(name="nbp", bufs=3))
+        grp = ctx.enter_context(tc.tile_pool(name="grp", bufs=4))
+        cdp = ctx.enter_context(tc.tile_pool(name="cdp", bufs=3))
+        osp = ctx.enter_context(tc.tile_pool(name="osp", bufs=3))
+        tps = ctx.enter_context(tc.psum_pool(name="tps", bufs=6))
+        ops = ctx.enter_context(tc.psum_pool(name="ops", bufs=2))
+        ctx.enter_context(tc.manual_schedule())
+
+        mf = const.tile([P, I * M * 2], BF16)
+        nc.scalar.dma_start(out=mf[:], in_=mfs.rearrange("i m c -> (i m c)").partition_broadcast(P))
+        xs = const.tile([P, NJ * I], BF16)
+        nc.sync.dma_start(out=xs[:], in_=x.rearrange("(p j) i -> p (j i)", j=NJ))
+        rl = const.tile([P, 4, O], BF16)
+        nc.sync.dma_start(out=rl[:], in_=rules.rearrange("(p t) o -> p t o", t=4))
+
+        ident = const.tile([P, P], BF16)
+        make_identity(nc, ident[:])
+
+        mfv = mf[:].rearrange("p (k c) -> p k c", c=2)
+        mean = const.tile([P, I * M], F32)
+        nc.vector.tensor_copy(out=mean[:], in_=mfv[:, :, 0])
+        sg = const.tile([P, I * M], F32)
+        nc.scalar.activation(out=sg[:], in_=mfv[:, :, 1], func=ACT.Abs)
+        nc.vector.tensor_scalar_add(out=sg[:], in0=sg[:], scalar1=EPS)
+        rs = const.tile([P, I * M], F32)
+        nc.vector.reciprocal(out=rs[:], in_=sg[:])
+
+        rg = const.tile([P, O, 4], BF16, align_bytes=64)
+        rcodes = const.tile([P, O], U32, align_bytes=64)
+        rscales = const.tile([P, O], U8, align_bytes=64)
+
+        out_v = out.rearrange("(p j) o -> p j o", j=NJ)
+
+        def make_chunk(j0, cj):
+            z = small.tile([P, cj, I, M], F32, tag="z", name="z")
+            mb = small.tile([P, cj, I, M], F32, tag="mb", name="mb")
+            s = small.tile([P, cj, I], F32, tag="s", name="s")
+            t4 = small.tile([P, cj, 4], F32, tag="t4", name="t4")
+            t2 = small.tile([P, cj, 2], F32, tag="t2", name="t2")
+            t1 = small.tile([P, cj, 1], F32, tag="t1", name="t1")
+            rinv = small.tile([P, cj, 1], F32, tag="rinv", name="rinv")
+            m7r = small.tile([P, cj, M], F32, tag="m7r", name="m7r")
+            h = small.tile([P, cj, 2, 2], F32, tag="h", name="h")
+            a01 = small.tile([P, cj, 2, 2], F32, tag="a01", name="a01")
+            a = small.tile([P, cj, 4, 2], F32, tag="a", name="a")
+            b34 = small.tile([P, cj, 2, 2], F32, tag="b34", name="b34")
+            b56 = small.tile([P, cj, 2, 2], F32, tag="b56", name="b56")
+            bb = small.tile([P, cj, 4, 4], F32, tag="bb", name="bb")
+            s7 = s7p.tile([P, cj, 8, 16], F32, tag="s7", name="s7")
+            xv = xs[:, j0 * I : (j0 + cj) * I].rearrange("p (j i) -> p j i", i=I)
+            full = [P, cj, I, M]
+
+            def tt(o, i0, i1, op):
+                return lambda: nc.vector.tensor_tensor(out=o, in0=i0, in1=i1, op=op)
+
+            def outer(o, u, nu, v, nv):
+                return tt(
+                    o[:],
+                    u.unsqueeze(3).to_broadcast([P, cj, nu, nv]),
+                    v.unsqueeze(2).to_broadcast([P, cj, nu, nv]),
+                    ALU.mult,
+                )
+
+            def flat(t):
+                return t[:].rearrange("p j a b -> p j (a b)")
+
+            v0 = [
+                tt(
+                    z[:],
+                    xv.unsqueeze(3).to_broadcast(full),
+                    mean[:].rearrange("p (i m) -> p i m", m=M).unsqueeze(1).to_broadcast(full),
+                    ALU.subtract,
+                ),
+                tt(z[:], z[:], rs[:].rearrange("p (i m) -> p i m", m=M).unsqueeze(1).to_broadcast(full), ALU.mult),
+            ]
+            sc = [
+                lambda: nc.scalar.activation(out=mb[:], in_=z[:], func=ACT.Square),
+                lambda: nc.scalar.activation(out=mb[:], in_=mb[:], func=ACT.Exp, scale=-0.5),
+            ]
+            rest = [
+                outer(a01, mb[:, :, 0, :], 2, mb[:, :, 1, :], 2),
+                outer(b34, mb[:, :, 3, :], 2, mb[:, :, 4, :], 2),
+                outer(b56, mb[:, :, 5, :], 2, mb[:, :, 6, :], 2),
+                tt(s[:], mb[:, :, :, 0], mb[:, :, :, 1], ALU.add),
+                outer(a, flat(a01), 4, mb[:, :, 2, :], 2),
+                tt(t4[:], s[:, :, 0:4], s[:, :, 4:8], ALU.mult),
+                outer(bb, flat(b34), 4, flat(b56), 4),
+                tt(t2[:], t4[:, :, 0:2], t4[:, :, 2:4], ALU.mult),
+                tt(t1[:], t2[:, :, 0:1], t2[:, :, 1:2], ALU.mult),
+                tt(t1[:], t1[:], s[:, :, 8:9], ALU.mult),
+                lambda: nc.vector.tensor_scalar_add(out=t1[:], in0=t1[:], scalar1=EPS),
+                lambda: nc.vector.reciprocal(out=rinv[:], in_=t1[:]),
+                tt(m7r[:], mb[:, :, 7, :], rinv[:].to_broadcast([P, cj, M]), ALU.mult),
+                outer(h, m7r[:], 2, mb[:, :, 8, :], 2),
+            ]
+
+            def s7piece(q0):
+                nc.vector.tensor_tensor(
+                    out=s7[:, q0 : q0 + QUAD, :, :],
+                    in0=flat(a)[:, q0 : q0 + QUAD, :].unsqueeze(3).to_broadcast([P, QUAD, 8, 16]),
+                    in1=flat(bb)[:, q0 : q0 + QUAD, :].unsqueeze(2).to_broadcast([P, QUAD, 8, 16]),
+                    op=ALU.mult,
+                )
+
+            return {
+                "v0": v0,
+                "sc": sc,
+                "rest": rest,
+                "s7piece": s7piece,
+                "s7v": s7[:].rearrange("p j a b -> p j (a b)"),
+                "hv": h[:].rearrange("p j a b -> p (j a b)"),
+            }
+
+        quad_info = []
+        starts = []
+        j0 = 0
+        for c, cj in enumerate(CHUNKS):
+            starts.append(j0)
+            for q0 in range(0, cj, QUAD):
+                quad_info.append((c, q0, cj // QUAD))
+            j0 += cj
+
+        chunks = {0: make_chunk(0, CHUNKS[0])}
+        for f in chunks[0]["v0"] + chunks[0]["sc"] + chunks[0]["rest"]:
+            f()
+        chunks[0]["s7piece"](0)
+
+        nbs, gs, cds, pos, osts = {}, {}, {}, {}, {}
+        pending = []
+        for s in range(NQ + LAG):
+            if s < NQ:
+                c, q0, nquads = quad_info[s]
+                ch = chunks[c]
+                if q0 == 0 and c + 1 < len(CHUNKS):
+                    chunks[c + 1] = make_chunk(starts[c + 1], CHUNKS[c + 1])
+                    for f in chunks[c + 1]["v0"] + chunks[c + 1]["sc"]:
+                        f()
+                    pending = list(chunks[c + 1]["rest"])
+                nb = nbp.tile([P, QUAD, 4, P], BF16, tag="nb", name="nb")
+                for jj in range(QUAD):
+                    jl = q0 + jj
+                    for t in range(4):
+                        nc.vector.tensor_scalar(
+                            out=nb[:, jj, t, :],
+                            in0=ch["s7v"][:, jl, :],
+                            scalar1=ch["hv"][:, jl * 4 + t : jl * 4 + t + 1],
+                            scalar2=None,
+                            op0=ALU.mult,
+                        )
+                tpl = []
+                for half in range(QUAD // 2):
+                    tp = tps.tile([P, 2, 4, P], BF16, tag="tp", name="tp")
+                    for k in range(2):
+                        for t in range(4):
+                            nc.tensor.transpose(tp[:, k, t, :], nb[:, half * 2 + k, t, :], ident[:])
+                    tpl.append(tp)
+            if s == 0:
+                nc.vector.tensor_copy(out=rg[:], in_=rl[:].rearrange("p t o -> p o t"))
+            if s >= LAG:
+                g = gs[s - LAG]
+                codes = cdp.tile([P, QUAD * P], U32, tag="codes", name="codes", align_bytes=64)
+                scales = cdp.tile([P, QUAD * P], U8, tag="scales", name="scales", align_bytes=64)
+                nc.vector.quantize_mx(
+                    out=codes[:].bitcast(FP8X4), scales=scales[:], in_=g[:].rearrange("p k b t -> p (k b t)")
+                )
+                po = ops.tile([P, QUAD, O], F32, tag="po", name="po")
+                for jj in range(QUAD):
+                    nc.tensor.matmul_mx(
+                        out=po[:, jj, :],
+                        lhsT=codes[:, jj * P : (jj + 1) * P].bitcast(FP8X4),
+                        lhsT_scale=scales[:, jj * P : (jj + 1) * P],
+                        rhs=rcodes[:].bitcast(FP8X4),
+                        rhs_scale=rscales[:],
+                        start=True,
+                        stop=True,
+                    )
+            if s < NQ:
+                g = grp.tile([P, QUAD, P, 4], BF16, tag="g", name="g", align_bytes=64)
+                gs[s] = g
+                for half in range(QUAD // 2):
+                    nc.scalar.copy(
+                        out=g[:, half * 2 : half * 2 + 2, :, :], in_=tpl[half][:].rearrange("p k t b -> p k b t")
+                    )
+            if s >= LAG:
+                sq = s - LAG
+                grp_i, pos_i = sq // GROUP, sq % GROUP
+                if pos_i == 0:
+                    osts[grp_i] = osp.tile([P, GROUP * QUAD, O], F32, tag="ost", name="ost")
+                ost = osts[grp_i]
+                nc.scalar.copy(out=ost[:, pos_i * QUAD : (pos_i + 1) * QUAD, :], in_=po[:])
+                last_group = grp_i == NQ // GROUP - 1
+                if last_group:
+                    nc.sync.dma_start(
+                        out=out_v[:, sq * QUAD : (sq + 1) * QUAD, :], in_=ost[:, pos_i * QUAD : (pos_i + 1) * QUAD, :]
+                    )
+                elif pos_i == GROUP - 1:
+                    nc.sync.dma_start(
+                        out=out_v[:, grp_i * GROUP * QUAD : (grp_i + 1) * GROUP * QUAD, :], in_=ost[:]
+                    )
+            if s == 0:
+                nc.vector.quantize_mx(
+                    out=rcodes[:].bitcast(FP8X4), scales=rscales[:], in_=rg[:].rearrange("p o t -> p (o t)")
+                )
+            if s < NQ:
+                left = nquads - q0 // QUAD
+                take = (len(pending) + left - 1) // left
+                if q0 == 0 and nquads > 1:
+                    take = 0
+                for f in pending[:take]:
+                    f()
+                pending = pending[take:]
+                if s + 1 < NQ:
+                    c1, q1, n1 = quad_info[s + 1]
+                    chunks[c1]["s7piece"](q1)

@@ -22,6 +22,7 @@ QUAD = 4
 NQ = NJ // QUAD
 GROUP = 4
 LAG = 2
+O_ON_VECTOR = 4
 
 
 def tile_extendedanfis_t_kernel(tc, x, mfs, rules, out):
@@ -71,7 +72,7 @@ def tile_extendedanfis_t_kernel(tc, x, mfs, rules, out):
             t2 = small.tile([P, cj, 2], F32, tag="t2", name="t2")
             t1 = small.tile([P, cj, 1], F32, tag="t1", name="t1")
             rinv = small.tile([P, cj, 1], F32, tag="rinv", name="rinv")
-            m7r = small.tile([P, cj, M], F32, tag="m7r", name="m7r")
+            h0 = small.tile([P, cj, 2, 2], F32, tag="h0", name="h0")
             h = small.tile([P, cj, 2, 2], F32, tag="h", name="h")
             a01 = small.tile([P, cj, 2, 2], F32, tag="a01", name="a01")
             a = small.tile([P, cj, 4, 2], F32, tag="a", name="a")
@@ -112,25 +113,25 @@ def tile_extendedanfis_t_kernel(tc, x, mfs, rules, out):
             rest = [
                 outer(a01, mb[:, :, 0, :], 2, mb[:, :, 1, :], 2),
                 outer(b34, mb[:, :, 3, :], 2, mb[:, :, 4, :], 2),
-                outer(b56, mb[:, :, 5, :], 2, mb[:, :, 6, :], 2),
                 tt(s[:], mb[:, :, :, 0], mb[:, :, :, 1], ALU.add),
+                outer(b56, mb[:, :, 5, :], 2, mb[:, :, 6, :], 2),
                 outer(a, flat(a01), 4, mb[:, :, 2, :], 2),
                 tt(t4[:], s[:, :, 0:4], s[:, :, 4:8], ALU.mult),
                 outer(bb, flat(b34), 4, flat(b56), 4),
                 tt(t2[:], t4[:, :, 0:2], t4[:, :, 2:4], ALU.mult),
+                outer(h0, mb[:, :, 7, :], 2, mb[:, :, 8, :], 2),
                 tt(t1[:], t2[:, :, 0:1], t2[:, :, 1:2], ALU.mult),
                 tt(t1[:], t1[:], s[:, :, 8:9], ALU.mult),
                 lambda: nc.vector.tensor_scalar_add(out=t1[:], in0=t1[:], scalar1=EPS),
                 lambda: nc.vector.reciprocal(out=rinv[:], in_=t1[:]),
-                tt(m7r[:], mb[:, :, 7, :], rinv[:].to_broadcast([P, cj, M]), ALU.mult),
-                outer(h, m7r[:], 2, mb[:, :, 8, :], 2),
+                tt(flat(h), flat(h0), rinv[:].to_broadcast([P, cj, 4]), ALU.mult),
             ]
 
-            def s7piece(q0):
+            def s7piece(q0, n=QUAD):
                 nc.vector.tensor_tensor(
-                    out=s7[:, q0 : q0 + QUAD, :, :],
-                    in0=flat(a)[:, q0 : q0 + QUAD, :].unsqueeze(3).to_broadcast([P, QUAD, 8, 16]),
-                    in1=flat(bb)[:, q0 : q0 + QUAD, :].unsqueeze(2).to_broadcast([P, QUAD, 8, 16]),
+                    out=s7[:, q0 : q0 + n, :, :],
+                    in0=flat(a)[:, q0 : q0 + n, :].unsqueeze(3).to_broadcast([P, n, 8, 16]),
+                    in1=flat(bb)[:, q0 : q0 + n, :].unsqueeze(2).to_broadcast([P, n, 8, 16]),
                     op=ALU.mult,
                 )
 
@@ -153,32 +154,77 @@ def tile_extendedanfis_t_kernel(tc, x, mfs, rules, out):
             j0 += cj
 
         chunks = {0: make_chunk(0, CHUNKS[0])}
-        for f in chunks[0]["v0"] + chunks[0]["sc"] + chunks[0]["rest"]:
+        for f in chunks[0]["v0"] + chunks[0]["sc"] + chunks[0]["rest"][:-4]:
             f()
-        chunks[0]["s7piece"](0)
+        for k, f in enumerate(chunks[0]["rest"][-4:]):
+            f()
+            chunks[0]["s7piece"](k, 1)
 
         nbs, gs, cds, pos, osts = {}, {}, {}, {}, {}
         pending = []
+        def s7_of(sn):
+            c1, q1, n1 = quad_info[sn]
+            return lambda: chunks[c1]["s7piece"](q1)
+
+        def quantise_of(sq):
+            def go():
+                codes = cdp.tile([P, QUAD * P], U32, tag="codes", name="codes", align_bytes=64)
+                scales = cdp.tile([P, QUAD * P], U8, tag="scales", name="scales", align_bytes=64)
+                cds[sq] = (codes, scales)
+                nc.vector.quantize_mx(
+                    out=codes[:].bitcast(FP8X4),
+                    scales=scales[:],
+                    in_=gs[sq][:].rearrange("p k b t -> p (k b t)"),
+                )
+
+            return go
+
         for s in range(NQ + LAG):
+            extras = []
+            scalar_ops = []
             if s < NQ:
                 c, q0, nquads = quad_info[s]
                 ch = chunks[c]
                 if q0 == 0 and c + 1 < len(CHUNKS):
                     chunks[c + 1] = make_chunk(starts[c + 1], CHUNKS[c + 1])
-                    for f in chunks[c + 1]["v0"] + chunks[c + 1]["sc"]:
-                        f()
+                    extras.extend(chunks[c + 1]["v0"])
+                    scalar_ops = chunks[c + 1]["sc"]
                     pending = list(chunks[c + 1]["rest"])
+                left = nquads - q0 // QUAD
+                take = (len(pending) + left - 1) // left
+                if q0 == 0 and nquads > 1:
+                    take = 0
+                if nquads > 1:
+                    extras.extend(pending[:take])
+                    pending = pending[take:]
+                    if s + 1 < NQ:
+                        extras.append(s7_of(s + 1))
+                if s >= LAG:
+                    extras.append(quantise_of(s - LAG))
                 nb = nbp.tile([P, QUAD, 4, P], BF16, tag="nb", name="nb")
-                for jj in range(QUAD):
+                n_f = QUAD * 4
+                done = 0
+                for k in range(n_f):
+                    jj, t = k // 4, k % 4
                     jl = q0 + jj
-                    for t in range(4):
-                        nc.vector.tensor_scalar(
-                            out=nb[:, jj, t, :],
-                            in0=ch["s7v"][:, jl, :],
-                            scalar1=ch["hv"][:, jl * 4 + t : jl * 4 + t + 1],
-                            scalar2=None,
-                            op0=ALU.mult,
-                        )
+                    nc.vector.tensor_scalar(
+                        out=nb[:, jj, t, :],
+                        in0=ch["s7v"][:, jl, :],
+                        scalar1=ch["hv"][:, jl * 4 + t : jl * 4 + t + 1],
+                        scalar2=None,
+                        op0=ALU.mult,
+                    )
+                    want = ((k + 1) * len(extras)) // n_f
+                    for f in extras[done:want]:
+                        f()
+                    done = want
+                for f in scalar_ops:
+                    f()
+                if nquads == 1:
+                    for f in pending:
+                        f()
+                    pending = []
+                    s7_of(s + 1)()
                 tpl = []
                 for half in range(QUAD // 2):
                     tp = tps.tile([P, 2, 4, P], BF16, tag="tp", name="tp")
@@ -189,12 +235,9 @@ def tile_extendedanfis_t_kernel(tc, x, mfs, rules, out):
             if s == 0:
                 nc.vector.tensor_copy(out=rg[:], in_=rl[:].rearrange("p t o -> p o t"))
             if s >= LAG:
-                g = gs[s - LAG]
-                codes = cdp.tile([P, QUAD * P], U32, tag="codes", name="codes", align_bytes=64)
-                scales = cdp.tile([P, QUAD * P], U8, tag="scales", name="scales", align_bytes=64)
-                nc.vector.quantize_mx(
-                    out=codes[:].bitcast(FP8X4), scales=scales[:], in_=g[:].rearrange("p k b t -> p (k b t)")
-                )
+                if s >= NQ:
+                    quantise_of(s - LAG)()
+                codes, scales = cds[s - LAG]
                 po = ops.tile([P, QUAD, O], F32, tag="po", name="po")
                 for jj in range(QUAD):
                     nc.tensor.matmul_mx(
@@ -210,16 +253,24 @@ def tile_extendedanfis_t_kernel(tc, x, mfs, rules, out):
                 g = grp.tile([P, QUAD, P, 4], BF16, tag="g", name="g", align_bytes=64)
                 gs[s] = g
                 for half in range(QUAD // 2):
-                    nc.scalar.copy(
-                        out=g[:, half * 2 : half * 2 + 2, :, :], in_=tpl[half][:].rearrange("p k t b -> p k b t")
-                    )
+                    if s == NQ - 1 and half == 1:
+                        nc.vector.tensor_copy(
+                            out=g[:, half * 2 : half * 2 + 2, :, :], in_=tpl[half][:].rearrange("p k t b -> p k b t")
+                        )
+                    else:
+                        nc.scalar.copy(
+                            out=g[:, half * 2 : half * 2 + 2, :, :], in_=tpl[half][:].rearrange("p k t b -> p k b t")
+                        )
             if s >= LAG:
                 sq = s - LAG
                 grp_i, pos_i = sq // GROUP, sq % GROUP
                 if pos_i == 0:
                     osts[grp_i] = osp.tile([P, GROUP * QUAD, O], F32, tag="ost", name="ost")
                 ost = osts[grp_i]
-                nc.scalar.copy(out=ost[:, pos_i * QUAD : (pos_i + 1) * QUAD, :], in_=po[:])
+                if sq % O_ON_VECTOR == O_ON_VECTOR - 1 or sq >= NQ - 2:
+                    nc.vector.tensor_copy(out=ost[:, pos_i * QUAD : (pos_i + 1) * QUAD, :], in_=po[:])
+                else:
+                    nc.scalar.copy(out=ost[:, pos_i * QUAD : (pos_i + 1) * QUAD, :], in_=po[:])
                 last_group = grp_i == NQ // GROUP - 1
                 if last_group:
                     nc.sync.dma_start(
@@ -233,14 +284,3 @@ def tile_extendedanfis_t_kernel(tc, x, mfs, rules, out):
                 nc.vector.quantize_mx(
                     out=rcodes[:].bitcast(FP8X4), scales=rscales[:], in_=rg[:].rearrange("p o t -> p (o t)")
                 )
-            if s < NQ:
-                left = nquads - q0 // QUAD
-                take = (len(pending) + left - 1) // left
-                if q0 == 0 and nquads > 1:
-                    take = 0
-                for f in pending[:take]:
-                    f()
-                pending = pending[take:]
-                if s + 1 < NQ:
-                    c1, q1, n1 = quad_info[s + 1]
-                    chunks[c1]["s7piece"](q1)

@@ -22,7 +22,7 @@ QUAD = 4
 NQ = NJ // QUAD
 GROUP = 4
 LAG = 2
-O_ON_VECTOR = 4
+EXTRA = 1
 
 
 def tile_extendedanfis_t_kernel(tc, x, mfs, rules, out):
@@ -35,7 +35,8 @@ def tile_extendedanfis_t_kernel(tc, x, mfs, rules, out):
         grp = ctx.enter_context(tc.tile_pool(name="grp", bufs=4))
         cdp = ctx.enter_context(tc.tile_pool(name="cdp", bufs=3))
         osp = ctx.enter_context(tc.tile_pool(name="osp", bufs=3))
-        tps = ctx.enter_context(tc.psum_pool(name="tps", bufs=6))
+        tps = ctx.enter_context(tc.psum_pool(name="tps", bufs=5))
+        scr = ctx.enter_context(tc.psum_pool(name="scr", bufs=1))
         ops = ctx.enter_context(tc.psum_pool(name="ops", bufs=2))
         ctx.enter_context(tc.manual_schedule())
 
@@ -160,7 +161,8 @@ def tile_extendedanfis_t_kernel(tc, x, mfs, rules, out):
             f()
             chunks[0]["s7piece"](k, 1)
 
-        nbs, gs, cds, pos, osts = {}, {}, {}, {}, {}
+        spare = scr.tile([P, QUAD * P], F32)
+        gs, cds, osts = {}, {}, {}
         pending = []
         def s7_of(sn):
             c1, q1, n1 = quad_info[sn]
@@ -181,15 +183,19 @@ def tile_extendedanfis_t_kernel(tc, x, mfs, rules, out):
 
         for s in range(NQ + LAG):
             extras = []
+            first_extras = []
             scalar_ops = []
             if s < NQ:
                 c, q0, nquads = quad_info[s]
                 ch = chunks[c]
                 if q0 == 0 and c + 1 < len(CHUNKS):
                     chunks[c + 1] = make_chunk(starts[c + 1], CHUNKS[c + 1])
-                    extras.extend(chunks[c + 1]["v0"])
+                    first_extras = chunks[c + 1]["v0"]
                     scalar_ops = chunks[c + 1]["sc"]
                     pending = list(chunks[c + 1]["rest"])
+                if s >= LAG:
+                    extras.append(quantise_of(s - LAG))
+                extras.extend(first_extras)
                 left = nquads - q0 // QUAD
                 take = (len(pending) + left - 1) // left
                 if q0 == 0 and nquads > 1:
@@ -199,8 +205,6 @@ def tile_extendedanfis_t_kernel(tc, x, mfs, rules, out):
                     pending = pending[take:]
                     if s + 1 < NQ:
                         extras.append(s7_of(s + 1))
-                if s >= LAG:
-                    extras.append(quantise_of(s - LAG))
                 nb = nbp.tile([P, QUAD, 4, P], BF16, tag="nb", name="nb")
                 n_f = QUAD * 4
                 done = 0
@@ -225,30 +229,43 @@ def tile_extendedanfis_t_kernel(tc, x, mfs, rules, out):
                         f()
                     pending = []
                     s7_of(s + 1)()
-                tpl = []
-                for half in range(QUAD // 2):
-                    tp = tps.tile([P, 2, 4, P], BF16, tag="tp", name="tp")
-                    for k in range(2):
-                        for t in range(4):
-                            nc.tensor.transpose(tp[:, k, t, :], nb[:, half * 2 + k, t, :], ident[:])
-                    tpl.append(tp)
-            if s == 0:
-                nc.vector.tensor_copy(out=rg[:], in_=rl[:].rearrange("p t o -> p o t"))
             if s >= LAG:
                 if s >= NQ:
                     quantise_of(s - LAG)()
                 codes, scales = cds[s - LAG]
                 po = ops.tile([P, QUAD, O], F32, tag="po", name="po")
-                for jj in range(QUAD):
-                    nc.tensor.matmul_mx(
-                        out=po[:, jj, :],
-                        lhsT=codes[:, jj * P : (jj + 1) * P].bitcast(FP8X4),
-                        lhsT_scale=scales[:, jj * P : (jj + 1) * P],
-                        rhs=rcodes[:].bitcast(FP8X4),
-                        rhs_scale=rscales[:],
-                        start=True,
-                        stop=True,
-                    )
+            tpl = []
+            for half in range(QUAD // 2):
+                if s < NQ:
+                    tp = tps.tile([P, 2, 4, P], BF16, tag="tp", name="tp")
+                    for k in range(2):
+                        for t in range(4):
+                            nc.tensor.transpose(tp[:, k, t, :], nb[:, half * 2 + k, t, :], ident[:])
+                    tpl.append(tp)
+                if s >= LAG:
+                    for jj in range(half * 2, half * 2 + 2):
+                        nc.tensor.matmul_mx(
+                            out=po[:, jj, :],
+                            lhsT=codes[:, jj * P : (jj + 1) * P].bitcast(FP8X4),
+                            lhsT_scale=scales[:, jj * P : (jj + 1) * P],
+                            rhs=rcodes[:].bitcast(FP8X4),
+                            rhs_scale=rscales[:],
+                            start=True,
+                            stop=True,
+                        )
+                    if s < NQ:
+                        for e in range(EXTRA):
+                            nc.tensor.matmul_mx(
+                                out=spare[:],
+                                lhsT=rcodes[:].bitcast(FP8X4),
+                                lhsT_scale=rscales[:],
+                                rhs=codes[:].bitcast(FP8X4),
+                                rhs_scale=scales[:],
+                                start=True,
+                                stop=True,
+                            )
+            if s == 0:
+                nc.vector.tensor_copy(out=rg[:], in_=rl[:].rearrange("p t o -> p o t"))
             if s < NQ:
                 g = grp.tile([P, QUAD, P, 4], BF16, tag="g", name="g", align_bytes=64)
                 gs[s] = g
@@ -267,7 +284,7 @@ def tile_extendedanfis_t_kernel(tc, x, mfs, rules, out):
                 if pos_i == 0:
                     osts[grp_i] = osp.tile([P, GROUP * QUAD, O], F32, tag="ost", name="ost")
                 ost = osts[grp_i]
-                if sq % O_ON_VECTOR == O_ON_VECTOR - 1 or sq >= NQ - 2:
+                if sq >= NQ - 2:
                     nc.vector.tensor_copy(out=ost[:, pos_i * QUAD : (pos_i + 1) * QUAD, :], in_=po[:])
                 else:
                     nc.scalar.copy(out=ost[:, pos_i * QUAD : (pos_i + 1) * QUAD, :], in_=po[:])

@@ -22,7 +22,7 @@ QUAD = 4
 NQ = NJ // QUAD
 GROUP = 4
 LAG = 2
-EXTRA = 1
+EXTRA = 2
 
 
 def tile_extendedanfis_t_kernel(tc, x, mfs, rules, out):

@@ -162,7 +162,7 @@ def tile_extendedanfis_t_kernel(tc, x, mfs, rules, out):
             chunks[0]["s7piece"](k, 1)
 
         spare = scr.tile([P, QUAD * P], F32)
-        gs, cds, osts = {}, {}, {}
+        gs, cds, osts, pos, copied = {}, {}, {}, {}, {}
         pending = []
         def s7_of(sn):
             c1, q1, n1 = quad_info[sn]
@@ -181,7 +181,28 @@ def tile_extendedanfis_t_kernel(tc, x, mfs, rules, out):
 
             return go
 
-        for s in range(NQ + LAG):
+        def store(sq):
+            grp_i, pos_i = sq // GROUP, sq % GROUP
+            copied[grp_i] = copied.get(grp_i, 0) + 1
+            if grp_i == NQ // GROUP - 1:
+                nc.sync.dma_start(
+                    out=out_v[:, sq * QUAD : (sq + 1) * QUAD, :],
+                    in_=osts[grp_i][:, pos_i * QUAD : (pos_i + 1) * QUAD, :],
+                )
+            elif copied[grp_i] == GROUP:
+                nc.sync.dma_start(
+                    out=out_v[:, grp_i * GROUP * QUAD : (grp_i + 1) * GROUP * QUAD, :], in_=osts[grp_i][:]
+                )
+
+        def vector_out_of(sq):
+            def go():
+                grp_i, pos_i = sq // GROUP, sq % GROUP
+                nc.vector.tensor_copy(out=osts[grp_i][:, pos_i * QUAD : (pos_i + 1) * QUAD, :], in_=pos[sq][:])
+                store(sq)
+
+            return go
+
+        for s in range(NQ + LAG + 1):
             extras = []
             first_extras = []
             scalar_ops = []
@@ -196,6 +217,8 @@ def tile_extendedanfis_t_kernel(tc, x, mfs, rules, out):
                 if s >= LAG:
                     extras.append(quantise_of(s - LAG))
                 extras.extend(first_extras)
+                if s > LAG and (s - LAG - 1) % 2 == 1:
+                    extras.append(vector_out_of(s - LAG - 1))
                 left = nquads - q0 // QUAD
                 take = (len(pending) + left - 1) // left
                 if q0 == 0 and nquads > 1:
@@ -229,11 +252,14 @@ def tile_extendedanfis_t_kernel(tc, x, mfs, rules, out):
                         f()
                     pending = []
                     s7_of(s + 1)()
-            if s >= LAG:
+            if s >= NQ and (s - LAG - 1) % 2 == 1:
+                vector_out_of(s - LAG - 1)()
+            if LAG <= s < NQ + LAG:
                 if s >= NQ:
                     quantise_of(s - LAG)()
                 codes, scales = cds[s - LAG]
                 po = ops.tile([P, QUAD, O], F32, tag="po", name="po")
+                pos[s - LAG] = po
             tpl = []
             for half in range(QUAD // 2):
                 if s < NQ:
@@ -242,7 +268,7 @@ def tile_extendedanfis_t_kernel(tc, x, mfs, rules, out):
                         for t in range(4):
                             nc.tensor.transpose(tp[:, k, t, :], nb[:, half * 2 + k, t, :], ident[:])
                     tpl.append(tp)
-                if s >= LAG:
+                if LAG <= s < NQ + LAG:
                     for jj in range(half * 2, half * 2 + 2):
                         nc.tensor.matmul_mx(
                             out=po[:, jj, :],
@@ -278,25 +304,14 @@ def tile_extendedanfis_t_kernel(tc, x, mfs, rules, out):
                         nc.scalar.copy(
                             out=g[:, half * 2 : half * 2 + 2, :, :], in_=tpl[half][:].rearrange("p k t b -> p k b t")
                         )
-            if s >= LAG:
+            if LAG <= s < NQ + LAG:
                 sq = s - LAG
                 grp_i, pos_i = sq // GROUP, sq % GROUP
                 if pos_i == 0:
                     osts[grp_i] = osp.tile([P, GROUP * QUAD, O], F32, tag="ost", name="ost")
-                ost = osts[grp_i]
-                if sq >= NQ - 2:
-                    nc.vector.tensor_copy(out=ost[:, pos_i * QUAD : (pos_i + 1) * QUAD, :], in_=po[:])
-                else:
-                    nc.scalar.copy(out=ost[:, pos_i * QUAD : (pos_i + 1) * QUAD, :], in_=po[:])
-                last_group = grp_i == NQ // GROUP - 1
-                if last_group:
-                    nc.sync.dma_start(
-                        out=out_v[:, sq * QUAD : (sq + 1) * QUAD, :], in_=ost[:, pos_i * QUAD : (pos_i + 1) * QUAD, :]
-                    )
-                elif pos_i == GROUP - 1:
-                    nc.sync.dma_start(
-                        out=out_v[:, grp_i * GROUP * QUAD : (grp_i + 1) * GROUP * QUAD, :], in_=ost[:]
-                    )
+                if sq % 2 == 0:
+                    nc.scalar.copy(out=osts[grp_i][:, pos_i * QUAD : (pos_i + 1) * QUAD, :], in_=po[:])
+                    store(sq)
             if s == 0:
                 nc.vector.quantize_mx(
                     out=rcodes[:].bitcast(FP8X4), scales=rscales[:], in_=rg[:].rearrange("p o t -> p (o t)")

@@ -17,11 +17,12 @@ R = 512
 NJ = B // P
 EPS = 1e-6
 FLOPS = 2 * B * R * O
-CHUNKS = [4, 12] + [16] * 7
+CHUNKS = [4, 12, 16, 32, 32, 32]
 QUAD = 4
 NQ = NJ // QUAD
 GROUP = 4
 LAG = 2
+ON_SCALAR = [(2, 3), (3, 3)]
 EXTRA = 2
 
 
@@ -31,7 +32,7 @@ def tile_extendedanfis_t_kernel(tc, x, mfs, rules, out):
         const = ctx.enter_context(tc.tile_pool(name="const", bufs=1))
         small = ctx.enter_context(tc.tile_pool(name="small", bufs=2))
         s7p = ctx.enter_context(tc.tile_pool(name="s7p", bufs=2))
-        nbp = ctx.enter_context(tc.tile_pool(name="nbp", bufs=3))
+        nbp = ctx.enter_context(tc.tile_pool(name="nbp", bufs=4))
         grp = ctx.enter_context(tc.tile_pool(name="grp", bufs=4))
         cdp = ctx.enter_context(tc.tile_pool(name="cdp", bufs=3))
         osp = ctx.enter_context(tc.tile_pool(name="osp", bufs=3))
@@ -162,7 +163,7 @@ def tile_extendedanfis_t_kernel(tc, x, mfs, rules, out):
             chunks[0]["s7piece"](k, 1)
 
         spare = scr.tile([P, QUAD * P], F32)
-        gs, cds, osts, pos, copied = {}, {}, {}, {}, {}
+        gs, cds, osts, nbs = {}, {}, {}, {}
         pending = []
         def s7_of(sn):
             c1, q1, n1 = quad_info[sn]
@@ -181,28 +182,20 @@ def tile_extendedanfis_t_kernel(tc, x, mfs, rules, out):
 
             return go
 
-        def store(sq):
-            grp_i, pos_i = sq // GROUP, sq % GROUP
-            copied[grp_i] = copied.get(grp_i, 0) + 1
-            if grp_i == NQ // GROUP - 1:
-                nc.sync.dma_start(
-                    out=out_v[:, sq * QUAD : (sq + 1) * QUAD, :],
-                    in_=osts[grp_i][:, pos_i * QUAD : (pos_i + 1) * QUAD, :],
+        def scalar_share(sn):
+            c1, q1, n1 = quad_info[sn]
+            nbs[sn] = nbp.tile([P, QUAD, 4, P], BF16, tag="nb", name="nb")
+            for jj, t in ON_SCALAR:
+                jl = q1 + jj
+                nc.scalar.activation(
+                    out=nbs[sn][:, jj, t, :],
+                    in_=chunks[c1]["s7v"][:, jl, :],
+                    func=ACT.Copy,
+                    scale=chunks[c1]["hv"][:, jl * 4 + t : jl * 4 + t + 1],
                 )
-            elif copied[grp_i] == GROUP:
-                nc.sync.dma_start(
-                    out=out_v[:, grp_i * GROUP * QUAD : (grp_i + 1) * GROUP * QUAD, :], in_=osts[grp_i][:]
-                )
 
-        def vector_out_of(sq):
-            def go():
-                grp_i, pos_i = sq // GROUP, sq % GROUP
-                nc.vector.tensor_copy(out=osts[grp_i][:, pos_i * QUAD : (pos_i + 1) * QUAD, :], in_=pos[sq][:])
-                store(sq)
-
-            return go
-
-        for s in range(NQ + LAG + 1):
+        scalar_share(0)
+        for s in range(NQ + LAG):
             extras = []
             first_extras = []
             scalar_ops = []
@@ -217,8 +210,6 @@ def tile_extendedanfis_t_kernel(tc, x, mfs, rules, out):
                 if s >= LAG:
                     extras.append(quantise_of(s - LAG))
                 extras.extend(first_extras)
-                if s > LAG and (s - LAG - 1) % 2 == 1:
-                    extras.append(vector_out_of(s - LAG - 1))
                 left = nquads - q0 // QUAD
                 take = (len(pending) + left - 1) // left
                 if q0 == 0 and nquads > 1:
@@ -228,11 +219,11 @@ def tile_extendedanfis_t_kernel(tc, x, mfs, rules, out):
                     pending = pending[take:]
                     if s + 1 < NQ:
                         extras.append(s7_of(s + 1))
-                nb = nbp.tile([P, QUAD, 4, P], BF16, tag="nb", name="nb")
-                n_f = QUAD * 4
+                nb = nbs[s]
+                mine = [(jj, t) for jj in range(QUAD) for t in range(4) if (jj, t) not in ON_SCALAR]
+                n_f = len(mine)
                 done = 0
-                for k in range(n_f):
-                    jj, t = k // 4, k % 4
+                for k, (jj, t) in enumerate(mine):
                     jl = q0 + jj
                     nc.vector.tensor_scalar(
                         out=nb[:, jj, t, :],
@@ -252,14 +243,11 @@ def tile_extendedanfis_t_kernel(tc, x, mfs, rules, out):
                         f()
                     pending = []
                     s7_of(s + 1)()
-            if s >= NQ and (s - LAG - 1) % 2 == 1:
-                vector_out_of(s - LAG - 1)()
-            if LAG <= s < NQ + LAG:
+            if s >= LAG:
                 if s >= NQ:
                     quantise_of(s - LAG)()
                 codes, scales = cds[s - LAG]
                 po = ops.tile([P, QUAD, O], F32, tag="po", name="po")
-                pos[s - LAG] = po
             tpl = []
             for half in range(QUAD // 2):
                 if s < NQ:
@@ -268,7 +256,7 @@ def tile_extendedanfis_t_kernel(tc, x, mfs, rules, out):
                         for t in range(4):
                             nc.tensor.transpose(tp[:, k, t, :], nb[:, half * 2 + k, t, :], ident[:])
                     tpl.append(tp)
-                if LAG <= s < NQ + LAG:
+                if s >= LAG:
                     for jj in range(half * 2, half * 2 + 2):
                         nc.tensor.matmul_mx(
                             out=po[:, jj, :],
@@ -304,15 +292,28 @@ def tile_extendedanfis_t_kernel(tc, x, mfs, rules, out):
                         nc.scalar.copy(
                             out=g[:, half * 2 : half * 2 + 2, :, :], in_=tpl[half][:].rearrange("p k t b -> p k b t")
                         )
-            if LAG <= s < NQ + LAG:
+            if s >= LAG:
                 sq = s - LAG
                 grp_i, pos_i = sq // GROUP, sq % GROUP
                 if pos_i == 0:
                     osts[grp_i] = osp.tile([P, GROUP * QUAD, O], F32, tag="ost", name="ost")
-                if sq % 2 == 0:
-                    nc.scalar.copy(out=osts[grp_i][:, pos_i * QUAD : (pos_i + 1) * QUAD, :], in_=po[:])
-                    store(sq)
+                ost = osts[grp_i]
+                if sq >= NQ - 2:
+                    nc.vector.tensor_copy(out=ost[:, pos_i * QUAD : (pos_i + 1) * QUAD, :], in_=po[:])
+                else:
+                    nc.scalar.copy(out=ost[:, pos_i * QUAD : (pos_i + 1) * QUAD, :], in_=po[:])
+                last_group = grp_i == NQ // GROUP - 1
+                if last_group:
+                    nc.sync.dma_start(
+                        out=out_v[:, sq * QUAD : (sq + 1) * QUAD, :], in_=ost[:, pos_i * QUAD : (pos_i + 1) * QUAD, :]
+                    )
+                elif pos_i == GROUP - 1:
+                    nc.sync.dma_start(
+                        out=out_v[:, grp_i * GROUP * QUAD : (grp_i + 1) * GROUP * QUAD, :], in_=ost[:]
+                    )
             if s == 0:
                 nc.vector.quantize_mx(
                     out=rcodes[:].bitcast(FP8X4), scales=rscales[:], in_=rg[:].rearrange("p o t -> p (o t)")
                 )
+            if s + 1 < NQ:
+                scalar_share(s + 1)

@@ -22,7 +22,7 @@ QUAD = 4
 NQ = NJ // QUAD
 GROUP = 4
 LAG = 2
-ON_SCALAR = [(2, 3), (3, 3)]
+ON_SCALAR = [(3, 3)]
 EXTRA = 2
 
 

@@ -22,7 +22,7 @@ QUAD = 4
 NQ = NJ // QUAD
 GROUP = 4
 LAG = 2
-ON_SCALAR = [(3, 3)]
+ON_SCALAR = [(1, 3), (2, 3), (3, 3)]
 EXTRA = 2
 
 
@@ -48,7 +48,7 @@ def tile_extendedanfis_t_kernel(tc, x, mfs, rules, out):
         rl = const.tile([P, 4, O], BF16)
         nc.sync.dma_start(out=rl[:], in_=rules.rearrange("(p t) o -> p t o", t=4))
 
-        ident = const.tile([P, P], BF16)
+        ident = const.tile([P, P], F32)
         make_identity(nc, ident[:])
 
         mfv = mf[:].rearrange("p (k c) -> p k c", c=2)
@@ -76,10 +76,10 @@ def tile_extendedanfis_t_kernel(tc, x, mfs, rules, out):
             rinv = small.tile([P, cj, 1], F32, tag="rinv", name="rinv")
             h0 = small.tile([P, cj, 2, 2], F32, tag="h0", name="h0")
             h = small.tile([P, cj, 2, 2], F32, tag="h", name="h")
-            a01 = small.tile([P, cj, 2, 2], F32, tag="a01", name="a01")
-            a = small.tile([P, cj, 4, 2], F32, tag="a", name="a")
-            b34 = small.tile([P, cj, 2, 2], F32, tag="b34", name="b34")
-            b56 = small.tile([P, cj, 2, 2], F32, tag="b56", name="b56")
+            c23 = small.tile([P, cj, 2, 2], F32, tag="c23", name="c23")
+            a = small.tile([P, cj, 2, 4], F32, tag="a", name="a")
+            c45 = small.tile([P, cj, 2, 2], F32, tag="c45", name="c45")
+            c68 = small.tile([P, cj, 2, 2], F32, tag="c68", name="c68")
             bb = small.tile([P, cj, 4, 4], F32, tag="bb", name="bb")
             s7 = s7p.tile([P, cj, 8, 16], F32, tag="s7", name="s7")
             xv = xs[:, j0 * I : (j0 + cj) * I].rearrange("p (j i) -> p j i", i=I)
@@ -113,15 +113,15 @@ def tile_extendedanfis_t_kernel(tc, x, mfs, rules, out):
                 lambda: nc.scalar.activation(out=mb[:], in_=mb[:], func=ACT.Exp, scale=-0.5),
             ]
             rest = [
-                outer(a01, mb[:, :, 0, :], 2, mb[:, :, 1, :], 2),
-                outer(b34, mb[:, :, 3, :], 2, mb[:, :, 4, :], 2),
+                outer(c23, mb[:, :, 2, :], 2, mb[:, :, 3, :], 2),
+                outer(c45, mb[:, :, 4, :], 2, mb[:, :, 5, :], 2),
                 tt(s[:], mb[:, :, :, 0], mb[:, :, :, 1], ALU.add),
-                outer(b56, mb[:, :, 5, :], 2, mb[:, :, 6, :], 2),
-                outer(a, flat(a01), 4, mb[:, :, 2, :], 2),
+                outer(c68, mb[:, :, 6, :], 2, mb[:, :, 8, :], 2),
+                outer(a, mb[:, :, 7, :], 2, flat(c23), 4),
                 tt(t4[:], s[:, :, 0:4], s[:, :, 4:8], ALU.mult),
-                outer(bb, flat(b34), 4, flat(b56), 4),
+                outer(bb, flat(c45), 4, flat(c68), 4),
                 tt(t2[:], t4[:, :, 0:2], t4[:, :, 2:4], ALU.mult),
-                outer(h0, mb[:, :, 7, :], 2, mb[:, :, 8, :], 2),
+                outer(h0, mb[:, :, 0, :], 2, mb[:, :, 1, :], 2),
                 tt(t1[:], t2[:, :, 0:1], t2[:, :, 1:2], ALU.mult),
                 tt(t1[:], t1[:], s[:, :, 8:9], ALU.mult),
                 lambda: nc.vector.tensor_scalar_add(out=t1[:], in0=t1[:], scalar1=EPS),
@@ -142,7 +142,7 @@ def tile_extendedanfis_t_kernel(tc, x, mfs, rules, out):
                 "sc": sc,
                 "rest": rest,
                 "s7piece": s7piece,
-                "s7v": s7[:].rearrange("p j a b -> p j (a b)"),
+                "s7v": s7[:].rearrange("p j (e a) b -> p j e (a b)", e=2),
                 "hv": h[:].rearrange("p j a b -> p (j a b)"),
             }
 
@@ -184,12 +184,12 @@ def tile_extendedanfis_t_kernel(tc, x, mfs, rules, out):
 
         def scalar_share(sn):
             c1, q1, n1 = quad_info[sn]
-            nbs[sn] = nbp.tile([P, QUAD, 4, P], BF16, tag="nb", name="nb")
+            nbs[sn] = nbp.tile([P, QUAD, 2, 2 * P], BF16, tag="nb", name="nb", align_bytes=64)
             for jj, t in ON_SCALAR:
                 jl = q1 + jj
                 nc.scalar.activation(
-                    out=nbs[sn][:, jj, t, :],
-                    in_=chunks[c1]["s7v"][:, jl, :],
+                    out=nbs[sn][:, jj, :, 64 * t : 64 * t + 64],
+                    in_=chunks[c1]["s7v"][:, jl, :, :],
                     func=ACT.Copy,
                     scale=chunks[c1]["hv"][:, jl * 4 + t : jl * 4 + t + 1],
                 )
@@ -226,8 +226,8 @@ def tile_extendedanfis_t_kernel(tc, x, mfs, rules, out):
                 for k, (jj, t) in enumerate(mine):
                     jl = q0 + jj
                     nc.vector.tensor_scalar(
-                        out=nb[:, jj, t, :],
-                        in0=ch["s7v"][:, jl, :],
+                        out=nb[:, jj, :, 64 * t : 64 * t + 64],
+                        in0=ch["s7v"][:, jl, :, :],
                         scalar1=ch["hv"][:, jl * 4 + t : jl * 4 + t + 1],
                         scalar2=None,
                         op0=ALU.mult,
@@ -251,10 +251,10 @@ def tile_extendedanfis_t_kernel(tc, x, mfs, rules, out):
             tpl = []
             for half in range(QUAD // 2):
                 if s < NQ:
-                    tp = tps.tile([P, 2, 4, P], BF16, tag="tp", name="tp")
+                    tp = tps.tile([P, 2, 2, P], F32, tag="tp", name="tp")
                     for k in range(2):
-                        for t in range(4):
-                            nc.tensor.transpose(tp[:, k, t, :], nb[:, half * 2 + k, t, :], ident[:])
+                        for u in range(2):
+                            nc.tensor.transpose(tp[:, k, u, :], nb[:, half * 2 + k, u, :].bitcast(F32), ident[:])
                     tpl.append(tp)
                 if s >= LAG:
                     for jj in range(half * 2, half * 2 + 2):
@@ -286,11 +286,11 @@ def tile_extendedanfis_t_kernel(tc, x, mfs, rules, out):
                 for half in range(QUAD // 2):
                     if s == NQ - 1 and half == 1:
                         nc.vector.tensor_copy(
-                            out=g[:, half * 2 : half * 2 + 2, :, :], in_=tpl[half][:].rearrange("p k t b -> p k b t")
+                            out=g[:, half * 2 : half * 2 + 2, :, :].bitcast(F32), in_=tpl[half][:].rearrange("p k u b -> p k b u")
                         )
                     else:
                         nc.scalar.copy(
-                            out=g[:, half * 2 : half * 2 + 2, :, :], in_=tpl[half][:].rearrange("p k t b -> p k b t")
+                            out=g[:, half * 2 : half * 2 + 2, :, :].bitcast(F32), in_=tpl[half][:].rearrange("p k u b -> p k b u")
                         )
             if s >= LAG:
                 sq = s - LAG

@@ -21,9 +21,8 @@ CHUNKS = [4, 12, 16, 32, 32, 32]
 QUAD = 4
 NQ = NJ // QUAD
 GROUP = 4
-LAG = 2
-ON_SCALAR = [(1, 3), (2, 3), (3, 3)]
-EXTRA = 2
+ST = 3
+EXTRA = 4
 
 
 def tile_extendedanfis_t_kernel(tc, x, mfs, rules, out):
@@ -31,10 +30,9 @@ def tile_extendedanfis_t_kernel(tc, x, mfs, rules, out):
     with ExitStack() as ctx:
         const = ctx.enter_context(tc.tile_pool(name="const", bufs=1))
         small = ctx.enter_context(tc.tile_pool(name="small", bufs=2))
-        s7p = ctx.enter_context(tc.tile_pool(name="s7p", bufs=2))
-        nbp = ctx.enter_context(tc.tile_pool(name="nbp", bufs=4))
+        nbp = ctx.enter_context(tc.tile_pool(name="nbp", bufs=5))
         grp = ctx.enter_context(tc.tile_pool(name="grp", bufs=4))
-        cdp = ctx.enter_context(tc.tile_pool(name="cdp", bufs=3))
+        cdp = ctx.enter_context(tc.tile_pool(name="cdp", bufs=4))
         osp = ctx.enter_context(tc.tile_pool(name="osp", bufs=3))
         tps = ctx.enter_context(tc.psum_pool(name="tps", bufs=5))
         scr = ctx.enter_context(tc.psum_pool(name="scr", bufs=1))
@@ -52,13 +50,15 @@ def tile_extendedanfis_t_kernel(tc, x, mfs, rules, out):
         make_identity(nc, ident[:])
 
         mfv = mf[:].rearrange("p (k c) -> p k c", c=2)
-        mean = const.tile([P, I * M], F32)
-        nc.vector.tensor_copy(out=mean[:], in_=mfv[:, :, 0])
         sg = const.tile([P, I * M], F32)
         nc.scalar.activation(out=sg[:], in_=mfv[:, :, 1], func=ACT.Abs)
         nc.vector.tensor_scalar_add(out=sg[:], in0=sg[:], scalar1=EPS)
         rs = const.tile([P, I * M], F32)
         nc.vector.reciprocal(out=rs[:], in_=sg[:])
+        bs = const.tile([P, I * M], F32)
+        nc.vector.scalar_tensor_tensor(
+            out=bs[:], in0=mfv[:, :, 0], scalar=-1.0, in1=rs[:], op0=ALU.mult, op1=ALU.mult
+        )
 
         rg = const.tile([P, O, 4], BF16, align_bytes=64)
         rcodes = const.tile([P, O], U32, align_bytes=64)
@@ -67,83 +67,92 @@ def tile_extendedanfis_t_kernel(tc, x, mfs, rules, out):
         out_v = out.rearrange("(p j) o -> p j o", j=NJ)
 
         def make_chunk(j0, cj):
-            z = small.tile([P, cj, I, M], F32, tag="z", name="z")
-            mb = small.tile([P, cj, I, M], F32, tag="mb", name="mb")
-            s = small.tile([P, cj, I], F32, tag="s", name="s")
-            t4 = small.tile([P, cj, 4], F32, tag="t4", name="t4")
-            t2 = small.tile([P, cj, 2], F32, tag="t2", name="t2")
-            t1 = small.tile([P, cj, 1], F32, tag="t1", name="t1")
-            rinv = small.tile([P, cj, 1], F32, tag="rinv", name="rinv")
+            nq = cj // QUAD
+            z = small.tile([P, I * M, cj], F32, tag="z", name="z")
+            mb = small.tile([P, I, M, cj], F32, tag="mb", name="mb")
+            s = small.tile([P, I, cj], F32, tag="s", name="s")
+            t4 = small.tile([P, 4, cj], F32, tag="t4", name="t4")
+            t2 = small.tile([P, 2, cj], F32, tag="t2", name="t2")
+            t1 = small.tile([P, cj], F32, tag="t1", name="t1")
+            rinv = small.tile([P, cj], F32, tag="rinv", name="rinv")
             h0 = small.tile([P, cj, 2, 2], F32, tag="h0", name="h0")
-            h = small.tile([P, cj, 2, 2], F32, tag="h", name="h")
+            h = small.tile([P, cj, 4], F32, tag="h", name="h")
+            hx = small.tile([P, cj, 2, 4], F32, tag="hx", name="hx")
             c23 = small.tile([P, cj, 2, 2], F32, tag="c23", name="c23")
-            a = small.tile([P, cj, 2, 4], F32, tag="a", name="a")
             c45 = small.tile([P, cj, 2, 2], F32, tag="c45", name="c45")
             c68 = small.tile([P, cj, 2, 2], F32, tag="c68", name="c68")
-            bb = small.tile([P, cj, 4, 4], F32, tag="bb", name="bb")
-            s7 = s7p.tile([P, cj, 8, 16], F32, tag="s7", name="s7")
+            xt = small.tile([P, cj, 8, 4], F32, tag="xt", name="xt")
+            yt = small.tile([P, cj, 4, 4], F32, tag="yt", name="yt")
+            a = small.tile([P, nq, 2, 4], F32, tag="a", name="a")
+            s7 = small.tile([P, nq, 8, 16], F32, tag="s7", name="s7")
             xv = xs[:, j0 * I : (j0 + cj) * I].rearrange("p (j i) -> p j i", i=I)
-            full = [P, cj, I, M]
 
             def tt(o, i0, i1, op):
                 return lambda: nc.vector.tensor_tensor(out=o, in0=i0, in1=i1, op=op)
 
-            def outer(o, u, nu, v, nv):
+            def outer(o, u, v):
+                n, nu = u.shape[1], u.shape[2]
+                nv = v.shape[2]
                 return tt(
-                    o[:],
-                    u.unsqueeze(3).to_broadcast([P, cj, nu, nv]),
-                    v.unsqueeze(2).to_broadcast([P, cj, nu, nv]),
+                    o,
+                    u.unsqueeze(3).to_broadcast([P, n, nu, nv]),
+                    v.unsqueeze(2).to_broadcast([P, n, nu, nv]),
                     ALU.mult,
                 )
+
+            def mem(i):
+                return mb[:, i, :, :].rearrange("p m j -> p j m")
 
             def flat(t):
                 return t[:].rearrange("p j a b -> p j (a b)")
 
-            v0 = [
-                tt(
-                    z[:],
-                    xv.unsqueeze(3).to_broadcast(full),
-                    mean[:].rearrange("p (i m) -> p i m", m=M).unsqueeze(1).to_broadcast(full),
-                    ALU.subtract,
-                ),
-                tt(z[:], z[:], rs[:].rearrange("p (i m) -> p i m", m=M).unsqueeze(1).to_broadcast(full), ALU.mult),
-            ]
-            sc = [
-                lambda: nc.scalar.activation(out=mb[:], in_=z[:], func=ACT.Square),
-                lambda: nc.scalar.activation(out=mb[:], in_=mb[:], func=ACT.Exp, scale=-0.5),
-            ]
-            rest = [
-                outer(c23, mb[:, :, 2, :], 2, mb[:, :, 3, :], 2),
-                outer(c45, mb[:, :, 4, :], 2, mb[:, :, 5, :], 2),
-                tt(s[:], mb[:, :, :, 0], mb[:, :, :, 1], ALU.add),
-                outer(c68, mb[:, :, 6, :], 2, mb[:, :, 8, :], 2),
-                outer(a, mb[:, :, 7, :], 2, flat(c23), 4),
-                tt(t4[:], s[:, :, 0:4], s[:, :, 4:8], ALU.mult),
-                outer(bb, flat(c45), 4, flat(c68), 4),
-                tt(t2[:], t4[:, :, 0:2], t4[:, :, 2:4], ALU.mult),
-                outer(h0, mb[:, :, 0, :], 2, mb[:, :, 1, :], 2),
-                tt(t1[:], t2[:, :, 0:1], t2[:, :, 1:2], ALU.mult),
-                tt(t1[:], t1[:], s[:, :, 8:9], ALU.mult),
-                lambda: nc.vector.tensor_scalar_add(out=t1[:], in0=t1[:], scalar1=EPS),
-                lambda: nc.vector.reciprocal(out=rinv[:], in_=t1[:]),
-                tt(flat(h), flat(h0), rinv[:].to_broadcast([P, cj, 4]), ALU.mult),
-            ]
+            def own(v):
+                return v.rearrange("p (n q) k -> p n q k", q=QUAD)[:, :, ST, :]
 
-            def s7piece(q0, n=QUAD):
-                nc.vector.tensor_tensor(
-                    out=s7[:, q0 : q0 + n, :, :],
-                    in0=flat(a)[:, q0 : q0 + n, :].unsqueeze(3).to_broadcast([P, n, 8, 16]),
-                    in1=flat(bb)[:, q0 : q0 + n, :].unsqueeze(2).to_broadcast([P, n, 8, 16]),
-                    op=ALU.mult,
+            def square(k):
+                return lambda: nc.scalar.activation(
+                    out=z[:, k, :],
+                    in_=xv[:, :, k // M],
+                    func=ACT.Square,
+                    scale=rs[:, k : k + 1],
+                    bias=bs[:, k : k + 1],
                 )
 
+            sc = [square(k) for k in range(I * M)]
+            sc.append(
+                lambda: nc.scalar.activation(
+                    out=mb[:].rearrange("p i m j -> p (i m j)"),
+                    in_=z[:].rearrange("p k j -> p (k j)"),
+                    func=ACT.Exp,
+                    scale=-0.5,
+                )
+            )
+            rest = [
+                tt(s[:], mb[:, :, 0, :], mb[:, :, 1, :], ALU.add),
+                outer(c23[:], mem(2), mem(3)),
+                tt(t4[:], s[:, 0:4, :], s[:, 4:8, :], ALU.mult),
+                outer(c45[:], mem(4), mem(5)),
+                tt(t2[:], t4[:, 0:2, :], t4[:, 2:4, :], ALU.mult),
+                outer(c68[:], mem(6), mem(8)),
+                tt(t1[:], t2[:, 0, :], t2[:, 1, :], ALU.mult),
+                outer(h0[:], mem(0), mem(1)),
+                tt(t1[:], t1[:], s[:, 8, :], ALU.mult),
+                outer(yt[:], flat(c45), flat(c68)),
+                lambda: nc.vector.tensor_scalar_add(out=t1[:], in0=t1[:], scalar1=EPS),
+                outer(a[:], own(mem(7)), own(flat(c23))),
+                lambda: nc.vector.reciprocal(out=rinv[:], in_=t1[:]),
+                outer(s7[:], flat(a), own(flat(yt))),
+                tt(h[:], flat(h0), rinv[:].unsqueeze(2).to_broadcast([P, cj, 4]), ALU.mult),
+                outer(hx[:], mem(7), h[:]),
+                outer(xt[:], flat(hx), flat(c23)),
+            ]
             return {
-                "v0": v0,
                 "sc": sc,
                 "rest": rest,
-                "s7piece": s7piece,
-                "s7v": s7[:].rearrange("p j (e a) b -> p j e (a b)", e=2),
-                "hv": h[:].rearrange("p j a b -> p (j a b)"),
+                "x": flat(xt),
+                "y": flat(yt),
+                "s7": s7[:].rearrange("p j (e a) b -> p j e (a b)", e=2),
+                "h": h,
             }
 
         quad_info = []
@@ -155,165 +164,157 @@ def tile_extendedanfis_t_kernel(tc, x, mfs, rules, out):
                 quad_info.append((c, q0, cj // QUAD))
             j0 += cj
 
-        chunks = {0: make_chunk(0, CHUNKS[0])}
-        for f in chunks[0]["v0"] + chunks[0]["sc"] + chunks[0]["rest"][:-4]:
-            f()
-        for k, f in enumerate(chunks[0]["rest"][-4:]):
-            f()
-            chunks[0]["s7piece"](k, 1)
-
         spare = scr.tile([P, QUAD * P], F32)
-        gs, cds, osts, nbs = {}, {}, {}, {}
-        pending = []
-        def s7_of(sn):
-            c1, q1, n1 = quad_info[sn]
-            return lambda: chunks[c1]["s7piece"](q1)
+        chunks, nbs, gs, cds, pos, osts, tpl = {}, {}, {}, {}, {}, {}, {}
 
-        def quantise_of(sq):
+        def open_quad(sn):
+            nbs[sn] = nbp.tile([P, QUAD, 4 * P], BF16, tag="nb", name="nb", align_bytes=64)
+
+        def direct(sn, jj):
+            c, q0, n = quad_info[sn]
+            ch = chunks[c]
+
             def go():
-                codes = cdp.tile([P, QUAD * P], U32, tag="codes", name="codes", align_bytes=64)
-                scales = cdp.tile([P, QUAD * P], U8, tag="scales", name="scales", align_bytes=64)
-                cds[sq] = (codes, scales)
-                nc.vector.quantize_mx(
-                    out=codes[:].bitcast(FP8X4),
-                    scales=scales[:],
-                    in_=gs[sq][:].rearrange("p k b t -> p (k b t)"),
+                nc.vector.tensor_tensor(
+                    out=nbs[sn][:, jj, :].rearrange("p (a b) -> p a b", b=16),
+                    in0=ch["x"][:, q0 + jj, :].unsqueeze(2).to_broadcast([P, 32, 16]),
+                    in1=ch["y"][:, q0 + jj, :].unsqueeze(1).to_broadcast([P, 32, 16]),
+                    op=ALU.mult,
                 )
 
             return go
 
         def scalar_share(sn):
-            c1, q1, n1 = quad_info[sn]
-            nbs[sn] = nbp.tile([P, QUAD, 2, 2 * P], BF16, tag="nb", name="nb", align_bytes=64)
-            for jj, t in ON_SCALAR:
-                jl = q1 + jj
+            c, q0, n = quad_info[sn]
+            ch = chunks[c]
+            nbv = nbs[sn][:, ST, :].rearrange("p (e w) -> p e w", e=2)
+            for t in range(4):
                 nc.scalar.activation(
-                    out=nbs[sn][:, jj, :, 64 * t : 64 * t + 64],
-                    in_=chunks[c1]["s7v"][:, jl, :, :],
+                    out=nbv[:, :, 64 * t : 64 * t + 64],
+                    in_=ch["s7"][:, q0 // QUAD, :, :],
                     func=ACT.Copy,
-                    scale=chunks[c1]["hv"][:, jl * 4 + t : jl * 4 + t + 1],
+                    scale=ch["h"][:, q0 + ST, t : t + 1],
                 )
 
+        def quantise(sq):
+            codes = cdp.tile([P, QUAD * P], U32, tag="codes", name="codes", align_bytes=64)
+            scales = cdp.tile([P, QUAD * P], U8, tag="scales", name="scales", align_bytes=64)
+            cds[sq] = (codes, scales)
+            nc.vector.quantize_mx(
+                out=codes[:].bitcast(FP8X4), scales=scales[:], in_=gs[sq][:].rearrange("p k b t -> p (k b t)")
+            )
+
+        def transposes(sq):
+            nb = nbs[sq]
+            for half in range(2):
+                tp = tps.tile([P, 2, 2, P], F32, tag="tp", name="tp")
+                tpl[sq, half] = tp
+                for k in range(2):
+                    for u in range(2):
+                        words = nb[:, half * 2 + k, 2 * P * u : 2 * P * (u + 1)].bitcast(F32)
+                        nc.tensor.transpose(tp[:, k, u, :], words, ident[:])
+
+        def evacuate(sq, half, copy):
+            if half == 0:
+                gs[sq] = grp.tile([P, QUAD, P, 4], BF16, tag="g", name="g", align_bytes=64)
+            copy(
+                out=gs[sq][:, half * 2 : half * 2 + 2, :, :].bitcast(F32),
+                in_=tpl[sq, half][:].rearrange("p k u b -> p k b u"),
+            )
+
+        def multiply(sq, extra):
+            codes, scales = cds[sq]
+            po = ops.tile([P, QUAD, O], F32, tag="po", name="po")
+            pos[sq] = po
+            for jj in range(QUAD):
+                nc.tensor.matmul_mx(
+                    out=po[:, jj, :],
+                    lhsT=codes[:, jj * P : (jj + 1) * P].bitcast(FP8X4),
+                    lhsT_scale=scales[:, jj * P : (jj + 1) * P],
+                    rhs=rcodes[:].bitcast(FP8X4),
+                    rhs_scale=rscales[:],
+                    start=True,
+                    stop=True,
+                )
+            for e in range(extra):
+                nc.tensor.matmul_mx(
+                    out=spare[:],
+                    lhsT=rcodes[:].bitcast(FP8X4),
+                    lhsT_scale=rscales[:],
+                    rhs=codes[:].bitcast(FP8X4),
+                    rhs_scale=scales[:],
+                    start=True,
+                    stop=True,
+                )
+
+        def put_out(sq, copy):
+            grp_i, pos_i = sq // GROUP, sq % GROUP
+            if pos_i == 0:
+                osts[grp_i] = osp.tile([P, GROUP * QUAD, O], F32, tag="ost", name="ost")
+            ost = osts[grp_i]
+            copy(out=ost[:, pos_i * QUAD : (pos_i + 1) * QUAD, :], in_=pos[sq][:])
+            if grp_i == NQ // GROUP - 1:
+                nc.sync.dma_start(
+                    out=out_v[:, sq * QUAD : (sq + 1) * QUAD, :], in_=ost[:, pos_i * QUAD : (pos_i + 1) * QUAD, :]
+                )
+            elif pos_i == GROUP - 1:
+                nc.sync.dma_start(out=out_v[:, grp_i * GROUP * QUAD : (grp_i + 1) * GROUP * QUAD, :], in_=ost[:])
+
+        chunks[0] = make_chunk(0, CHUNKS[0])
+        for f in chunks[0]["sc"] + chunks[0]["rest"]:
+            f()
+        open_quad(0)
         scalar_share(0)
-        for s in range(NQ + LAG):
-            extras = []
-            first_extras = []
+        pending = []
+        for s in range(NQ + 4):
             scalar_ops = []
             if s < NQ:
-                c, q0, nquads = quad_info[s]
-                ch = chunks[c]
+                c, q0, n = quad_info[s]
+                extras = []
                 if q0 == 0 and c + 1 < len(CHUNKS):
                     chunks[c + 1] = make_chunk(starts[c + 1], CHUNKS[c + 1])
-                    first_extras = chunks[c + 1]["v0"]
                     scalar_ops = chunks[c + 1]["sc"]
                     pending = list(chunks[c + 1]["rest"])
-                if s >= LAG:
-                    extras.append(quantise_of(s - LAG))
-                extras.extend(first_extras)
-                left = nquads - q0 // QUAD
-                take = (len(pending) + left - 1) // left
-                if q0 == 0 and nquads > 1:
-                    take = 0
-                if nquads > 1:
-                    extras.extend(pending[:take])
+                if q0 > 0 and pending:
+                    left = max(1, n - 1 - q0 // QUAD)
+                    take = (len(pending) + left - 1) // left
+                    extras = pending[:take]
                     pending = pending[take:]
-                    if s + 1 < NQ:
-                        extras.append(s7_of(s + 1))
-                nb = nbs[s]
-                mine = [(jj, t) for jj in range(QUAD) for t in range(4) if (jj, t) not in ON_SCALAR]
-                n_f = len(mine)
-                done = 0
-                for k, (jj, t) in enumerate(mine):
-                    jl = q0 + jj
-                    nc.vector.tensor_scalar(
-                        out=nb[:, jj, :, 64 * t : 64 * t + 64],
-                        in0=ch["s7v"][:, jl, :, :],
-                        scalar1=ch["hv"][:, jl * 4 + t : jl * 4 + t + 1],
-                        scalar2=None,
-                        op0=ALU.mult,
-                    )
-                    want = ((k + 1) * len(extras)) // n_f
-                    for f in extras[done:want]:
+                if s == 0:
+                    for f in scalar_ops:
                         f()
-                    done = want
-                for f in scalar_ops:
+                    scalar_ops = []
+                work = [direct(s, jj) for jj in range(QUAD) if jj != ST]
+                if s >= 2:
+                    work.insert(1, lambda: quantise(s - 2))
+                done = 0
+                for k, f in enumerate(work):
                     f()
-                if nquads == 1:
+                    want = (k + 1) * len(extras) // len(work)
+                    for e in extras[done:want]:
+                        e()
+                    done = want
+                if s == 0:
+                    nc.vector.tensor_copy(out=rg[:], in_=rl[:].rearrange("p t o -> p o t"))
                     for f in pending:
                         f()
                     pending = []
-                    s7_of(s + 1)()
-            if s >= LAG:
-                if s >= NQ:
-                    quantise_of(s - LAG)()
-                codes, scales = cds[s - LAG]
-                po = ops.tile([P, QUAD, O], F32, tag="po", name="po")
-            tpl = []
-            for half in range(QUAD // 2):
-                if s < NQ:
-                    tp = tps.tile([P, 2, 2, P], F32, tag="tp", name="tp")
-                    for k in range(2):
-                        for u in range(2):
-                            nc.tensor.transpose(tp[:, k, u, :], nb[:, half * 2 + k, u, :].bitcast(F32), ident[:])
-                    tpl.append(tp)
-                if s >= LAG:
-                    for jj in range(half * 2, half * 2 + 2):
-                        nc.tensor.matmul_mx(
-                            out=po[:, jj, :],
-                            lhsT=codes[:, jj * P : (jj + 1) * P].bitcast(FP8X4),
-                            lhsT_scale=scales[:, jj * P : (jj + 1) * P],
-                            rhs=rcodes[:].bitcast(FP8X4),
-                            rhs_scale=rscales[:],
-                            start=True,
-                            stop=True,
-                        )
-                    if s < NQ:
-                        for e in range(EXTRA):
-                            nc.tensor.matmul_mx(
-                                out=spare[:],
-                                lhsT=rcodes[:].bitcast(FP8X4),
-                                lhsT_scale=rscales[:],
-                                rhs=codes[:].bitcast(FP8X4),
-                                rhs_scale=scales[:],
-                                start=True,
-                                stop=True,
-                            )
-            if s == 0:
-                nc.vector.tensor_copy(out=rg[:], in_=rl[:].rearrange("p t o -> p o t"))
-            if s < NQ:
-                g = grp.tile([P, QUAD, P, 4], BF16, tag="g", name="g", align_bytes=64)
-                gs[s] = g
-                for half in range(QUAD // 2):
-                    if s == NQ - 1 and half == 1:
-                        nc.vector.tensor_copy(
-                            out=g[:, half * 2 : half * 2 + 2, :, :].bitcast(F32), in_=tpl[half][:].rearrange("p k u b -> p k b u")
-                        )
-                    else:
-                        nc.scalar.copy(
-                            out=g[:, half * 2 : half * 2 + 2, :, :].bitcast(F32), in_=tpl[half][:].rearrange("p k u b -> p k b u")
-                        )
-            if s >= LAG:
-                sq = s - LAG
-                grp_i, pos_i = sq // GROUP, sq % GROUP
-                if pos_i == 0:
-                    osts[grp_i] = osp.tile([P, GROUP * QUAD, O], F32, tag="ost", name="ost")
-                ost = osts[grp_i]
-                if sq >= NQ - 2:
-                    nc.vector.tensor_copy(out=ost[:, pos_i * QUAD : (pos_i + 1) * QUAD, :], in_=po[:])
-                else:
-                    nc.scalar.copy(out=ost[:, pos_i * QUAD : (pos_i + 1) * QUAD, :], in_=po[:])
-                last_group = grp_i == NQ // GROUP - 1
-                if last_group:
-                    nc.sync.dma_start(
-                        out=out_v[:, sq * QUAD : (sq + 1) * QUAD, :], in_=ost[:, pos_i * QUAD : (pos_i + 1) * QUAD, :]
+                    nc.vector.quantize_mx(
+                        out=rcodes[:].bitcast(FP8X4), scales=rscales[:], in_=rg[:].rearrange("p o t -> p (o t)")
                     )
-                elif pos_i == GROUP - 1:
-                    nc.sync.dma_start(
-                        out=out_v[:, grp_i * GROUP * QUAD : (grp_i + 1) * GROUP * QUAD, :], in_=ost[:]
-                    )
-            if s == 0:
-                nc.vector.quantize_mx(
-                    out=rcodes[:].bitcast(FP8X4), scales=rscales[:], in_=rg[:].rearrange("p o t -> p (o t)")
-                )
+            elif s - 2 < NQ:
+                quantise(s - 2)
+            if 1 <= s <= NQ:
+                transposes(s - 1)
+            if 3 <= s < NQ + 3:
+                multiply(s - 3, EXTRA if s < NQ else 0)
             if s + 1 < NQ:
+                open_quad(s + 1)
                 scalar_share(s + 1)
+            if s >= 4:
+                put_out(s - 4, nc.scalar.copy)
+            if 1 <= s <= NQ:
+                for half in range(2):
+                    evacuate(s - 1, half, nc.scalar.copy)
+            for f in scalar_ops:
+                f()

@@ -17,12 +17,14 @@ R = 512
 NJ = B // P
 EPS = 1e-6
 FLOPS = 2 * B * R * O
-CHUNKS = [4, 12, 16, 32, 32, 32]
 QUAD = 4
 NQ = NJ // QUAD
+EARLY = [4, 12]
+NE = sum(EARLY)
+LATE = NJ - NE
+SUBS = [16, 32, 32, 32]
 GROUP = 4
-ST = 3
-EXTRA = 4
+EXTRA = 1
 
 
 def tile_extendedanfis_t_kernel(tc, x, mfs, rules, out):
@@ -30,12 +32,12 @@ def tile_extendedanfis_t_kernel(tc, x, mfs, rules, out):
     with ExitStack() as ctx:
         const = ctx.enter_context(tc.tile_pool(name="const", bufs=1))
         small = ctx.enter_context(tc.tile_pool(name="small", bufs=2))
-        nbp = ctx.enter_context(tc.tile_pool(name="nbp", bufs=5))
+        l7p = ctx.enter_context(tc.tile_pool(name="l7p", bufs=3))
+        nbp = ctx.enter_context(tc.tile_pool(name="nbp", bufs=4))
         grp = ctx.enter_context(tc.tile_pool(name="grp", bufs=4))
         cdp = ctx.enter_context(tc.tile_pool(name="cdp", bufs=4))
         osp = ctx.enter_context(tc.tile_pool(name="osp", bufs=3))
-        tps = ctx.enter_context(tc.psum_pool(name="tps", bufs=5))
-        scr = ctx.enter_context(tc.psum_pool(name="scr", bufs=1))
+        tps = ctx.enter_context(tc.psum_pool(name="tps", bufs=6))
         ops = ctx.enter_context(tc.psum_pool(name="ops", bufs=2))
         ctx.enter_context(tc.manual_schedule())
 
@@ -66,135 +68,176 @@ def tile_extendedanfis_t_kernel(tc, x, mfs, rules, out):
 
         out_v = out.rearrange("(p j) o -> p j o", j=NJ)
 
-        def make_chunk(j0, cj):
-            nq = cj // QUAD
-            z = small.tile([P, I * M, cj], F32, tag="z", name="z")
-            mb = small.tile([P, I, M, cj], F32, tag="mb", name="mb")
-            s = small.tile([P, I, cj], F32, tag="s", name="s")
-            t4 = small.tile([P, 4, cj], F32, tag="t4", name="t4")
-            t2 = small.tile([P, 2, cj], F32, tag="t2", name="t2")
-            t1 = small.tile([P, cj], F32, tag="t1", name="t1")
-            rinv = small.tile([P, cj], F32, tag="rinv", name="rinv")
-            h0 = small.tile([P, cj, 2, 2], F32, tag="h0", name="h0")
-            h = small.tile([P, cj, 4], F32, tag="h", name="h")
-            hx = small.tile([P, cj, 2, 4], F32, tag="hx", name="hx")
-            c23 = small.tile([P, cj, 2, 2], F32, tag="c23", name="c23")
-            c45 = small.tile([P, cj, 2, 2], F32, tag="c45", name="c45")
-            c68 = small.tile([P, cj, 2, 2], F32, tag="c68", name="c68")
-            xt = small.tile([P, cj, 8, 4], F32, tag="xt", name="xt")
-            yt = small.tile([P, cj, 4, 4], F32, tag="yt", name="yt")
-            a = small.tile([P, nq, 2, 4], F32, tag="a", name="a")
-            s7 = small.tile([P, nq, 8, 16], F32, tag="s7", name="s7")
+        def tt(o, i0, i1, op):
+            return lambda: nc.vector.tensor_tensor(out=o, in0=i0, in1=i1, op=op)
+
+        def outer(o, u, v, op=ALU.mult):
+            n, nu = u.shape[1], u.shape[2]
+            nv = v.shape[2]
+            return tt(
+                o,
+                u.unsqueeze(3).to_broadcast([P, n, nu, nv]),
+                v.unsqueeze(2).to_broadcast([P, n, nu, nv]),
+                op,
+            )
+
+        def flat(t):
+            return t[:].rearrange("p j a b -> p j (a b)")
+
+        def memberships(pool, pre, j0, cj):
+            z = pool.tile([P, I, M, cj], F32, tag=pre + "z", name=pre + "z")
+            mb = pool.tile([P, I, M, cj], F32, tag=pre + "mb", name=pre + "mb")
+            s = pool.tile([P, I, cj], F32, tag=pre + "s", name=pre + "s")
+            t4 = pool.tile([P, 4, cj], F32, tag=pre + "t4", name=pre + "t4")
+            t2 = pool.tile([P, 2, cj], F32, tag=pre + "t2", name=pre + "t2")
+            t1 = pool.tile([P, cj], F32, tag=pre + "t1", name=pre + "t1")
+            rinv = pool.tile([P, cj], F32, tag=pre + "rinv", name=pre + "rinv")
             xv = xs[:, j0 * I : (j0 + cj) * I].rearrange("p (j i) -> p j i", i=I)
 
-            def tt(o, i0, i1, op):
-                return lambda: nc.vector.tensor_tensor(out=o, in0=i0, in1=i1, op=op)
-
-            def outer(o, u, v):
-                n, nu = u.shape[1], u.shape[2]
-                nv = v.shape[2]
-                return tt(
-                    o,
-                    u.unsqueeze(3).to_broadcast([P, n, nu, nv]),
-                    v.unsqueeze(2).to_broadcast([P, n, nu, nv]),
-                    ALU.mult,
-                )
-
-            def mem(i):
-                return mb[:, i, :, :].rearrange("p m j -> p j m")
-
-            def flat(t):
-                return t[:].rearrange("p j a b -> p j (a b)")
-
-            def own(v):
-                return v.rearrange("p (n q) k -> p n q k", q=QUAD)[:, :, ST, :]
-
-            def square(k):
+            def square(i, m):
+                k = i * M + m
                 return lambda: nc.scalar.activation(
-                    out=z[:, k, :],
-                    in_=xv[:, :, k // M],
+                    out=z[:, i, m, :],
+                    in_=xv[:, :, i],
                     func=ACT.Square,
                     scale=rs[:, k : k + 1],
                     bias=bs[:, k : k + 1],
                 )
 
-            sc = [square(k) for k in range(I * M)]
-            sc.append(
-                lambda: nc.scalar.activation(
-                    out=mb[:].rearrange("p i m j -> p (i m j)"),
-                    in_=z[:].rearrange("p k j -> p (k j)"),
+            def exps(i0, i1):
+                return lambda: nc.scalar.activation(
+                    out=mb[:, i0:i1, :, :].rearrange("p i m j -> p (i m j)"),
+                    in_=z[:, i0:i1, :, :].rearrange("p i m j -> p (i m j)"),
                     func=ACT.Exp,
                     scale=-0.5,
                 )
-            )
-            rest = [
+
+            chain = [
                 tt(s[:], mb[:, :, 0, :], mb[:, :, 1, :], ALU.add),
-                outer(c23[:], mem(2), mem(3)),
                 tt(t4[:], s[:, 0:4, :], s[:, 4:8, :], ALU.mult),
-                outer(c45[:], mem(4), mem(5)),
                 tt(t2[:], t4[:, 0:2, :], t4[:, 2:4, :], ALU.mult),
-                outer(c68[:], mem(6), mem(8)),
                 tt(t1[:], t2[:, 0, :], t2[:, 1, :], ALU.mult),
-                outer(h0[:], mem(0), mem(1)),
                 tt(t1[:], t1[:], s[:, 8, :], ALU.mult),
-                outer(yt[:], flat(c45), flat(c68)),
                 lambda: nc.vector.tensor_scalar_add(out=t1[:], in0=t1[:], scalar1=EPS),
-                outer(a[:], own(mem(7)), own(flat(c23))),
                 lambda: nc.vector.reciprocal(out=rinv[:], in_=t1[:]),
-                outer(s7[:], flat(a), own(flat(yt))),
-                tt(h[:], flat(h0), rinv[:].unsqueeze(2).to_broadcast([P, cj, 4]), ALU.mult),
-                outer(hx[:], mem(7), h[:]),
-                outer(xt[:], flat(hx), flat(c23)),
             ]
             return {
-                "sc": sc,
-                "rest": rest,
-                "x": flat(xt),
-                "y": flat(yt),
-                "s7": s7[:].rearrange("p j (e a) b -> p j e (a b)", e=2),
-                "h": h,
+                "squares": [square(i, m) for i in range(I) for m in range(M)],
+                "exps": exps,
+                "chain": chain,
+                "z": z,
+                "mb": mb,
+                "sum": t1,
+                "rinv": rinv,
             }
 
-        quad_info = []
-        starts = []
-        j0 = 0
-        for c, cj in enumerate(CHUNKS):
-            starts.append(j0)
-            for q0 in range(0, cj, QUAD):
-                quad_info.append((c, q0, cj // QUAD))
-            j0 += cj
+        def product_tables(pre, n, mem, rinv):
+            h0 = small.tile([P, n, 2, 2], F32, tag=pre + "h0", name=pre + "h0")
+            h = small.tile([P, n, 4], F32, tag=pre + "h", name=pre + "h")
+            hx = small.tile([P, n, 2, 4], F32, tag=pre + "hx", name=pre + "hx")
+            c23 = small.tile([P, n, 2, 2], F32, tag=pre + "c23", name=pre + "c23")
+            c45 = small.tile([P, n, 2, 2], F32, tag=pre + "c45", name=pre + "c45")
+            c68 = small.tile([P, n, 2, 2], F32, tag=pre + "c68", name=pre + "c68")
+            xt = small.tile([P, n, 8, 4], F32, tag=pre + "xt", name=pre + "xt")
+            yt = small.tile([P, n, 4, 4], F32, tag=pre + "yt", name=pre + "yt")
+            ops_ = [
+                outer(h0[:], mem(0), mem(1)),
+                outer(c23[:], mem(2), mem(3)),
+                outer(c45[:], mem(4), mem(5)),
+                tt(h[:], flat(h0), rinv.unsqueeze(2).to_broadcast([P, n, 4]), ALU.mult),
+                outer(c68[:], mem(6), mem(8)),
+                outer(hx[:], mem(7), h[:]),
+                outer(yt[:], flat(c45), flat(c68)),
+                outer(xt[:], flat(hx), flat(c23)),
+            ]
+            return ops_, flat(xt), flat(yt)
 
-        spare = scr.tile([P, QUAD * P], F32)
-        chunks, nbs, gs, cds, pos, osts, tpl = {}, {}, {}, {}, {}, {}, {}
+        def log_tables(pre, n, sq, lns):
+            l01 = small.tile([P, n, 2, 2], F32, tag=pre + "l01", name=pre + "l01")
+            la = small.tile([P, n, 4, 2], F32, tag=pre + "la", name=pre + "la")
+            l34 = small.tile([P, n, 2, 2], F32, tag=pre + "l34", name=pre + "l34")
+            l56 = small.tile([P, n, 2, 2], F32, tag=pre + "l56", name=pre + "l56")
+            lb = small.tile([P, n, 4, 4], F32, tag=pre + "lb", name=pre + "lb")
+            l78 = small.tile([P, n, 2, 2], F32, tag=pre + "l78", name=pre + "l78")
+            lt = small.tile([P, n, 4], F32, tag=pre + "lt", name=pre + "lt")
+            ops_ = [
+                outer(l01[:], sq(0), sq(1), ALU.add),
+                outer(l34[:], sq(3), sq(4), ALU.add),
+                outer(l56[:], sq(5), sq(6), ALU.add),
+                outer(la[:], flat(l01), sq(2), ALU.add),
+                outer(l78[:], sq(7), sq(8), ALU.add),
+                outer(lb[:], flat(l34), flat(l56), ALU.add),
+            ]
+            last = [
+                lambda: nc.vector.scalar_tensor_tensor(
+                    out=lt[:],
+                    in0=lns.unsqueeze(2).to_broadcast([P, n, 4]),
+                    scalar=2.0,
+                    in1=flat(l78),
+                    op0=ALU.mult,
+                    op1=ALU.add,
+                )
+            ]
+            return ops_, last, flat(la), flat(lb), lt
 
-        def open_quad(sn):
-            nbs[sn] = nbp.tile([P, QUAD, 4 * P], BF16, tag="nb", name="nb", align_bytes=64)
+        def pick(t, i, j0, n, c):
+            return t[:, i, :, j0 : j0 + 2 * n].rearrange("p m (n c) -> p c n m", c=2)[:, c, :, :]
 
-        def direct(sn, jj):
-            c, q0, n = quad_info[sn]
-            ch = chunks[c]
+        nbs, l7s, gs, cds, pos, osts, tpl = {}, {}, {}, {}, {}, {}, {}
+        prod, logs = {}, {}
+
+        def early_tables(mem_chunk, s0, cj):
+            ops_ = []
+            for c in range(2):
+                o, xt, yt = product_tables(
+                    "e%d" % c,
+                    cj // 2,
+                    lambda i, c=c: pick(mem_chunk["mb"], i, 0, cj // 2, c),
+                    mem_chunk["rinv"][:].rearrange("p (n c) -> p c n", c=2)[:, c, :],
+                )
+                ops_.append(o)
+                for q in range(cj // QUAD):
+                    prod[s0 + q, c] = (xt, yt, 2 * q)
+            return [f for pair in zip(ops_[0], ops_[1]) for f in pair]
+
+        def late_tables(mem_chunk, lns, s0, j0, cj):
+            n = cj // 2
+            po, xt, yt = product_tables(
+                "l",
+                n,
+                lambda i: pick(mem_chunk["mb"], i, j0, n, 0),
+                mem_chunk["rinv"][:, j0 : j0 + cj].rearrange("p (n c) -> p c n", c=2)[:, 0, :],
+            )
+            lo, last, la, lb, lt = log_tables(
+                "l",
+                n,
+                lambda i: pick(mem_chunk["z"], i, j0, n, 1),
+                lns[:, j0 : j0 + cj].rearrange("p (n c) -> p c n", c=2)[:, 1, :],
+            )
+            for q in range(cj // QUAD):
+                prod[s0 + q, 0] = (xt, yt, 2 * q)
+                logs[s0 + q] = (la, lb, lt, 2 * q)
+            return [f for pair in zip(po, lo) for f in pair] + po[len(lo) :], last
+
+        def direct(s, c):
+            xt, yt, n = prod[s, c]
 
             def go():
                 nc.vector.tensor_tensor(
-                    out=nbs[sn][:, jj, :].rearrange("p (a b) -> p a b", b=16),
-                    in0=ch["x"][:, q0 + jj, :].unsqueeze(2).to_broadcast([P, 32, 16]),
-                    in1=ch["y"][:, q0 + jj, :].unsqueeze(1).to_broadcast([P, 32, 16]),
+                    out=nbs[s][:, 2 * c : 2 * c + 2, :].rearrange("p k (a b) -> p k a b", b=16),
+                    in0=xt[:, n : n + 2, :].unsqueeze(3).to_broadcast([P, 2, 32, 16]),
+                    in1=yt[:, n : n + 2, :].unsqueeze(2).to_broadcast([P, 2, 32, 16]),
                     op=ALU.mult,
                 )
 
             return go
 
-        def scalar_share(sn):
-            c, q0, n = quad_info[sn]
-            ch = chunks[c]
-            nbv = nbs[sn][:, ST, :].rearrange("p (e w) -> p e w", e=2)
-            for t in range(4):
-                nc.scalar.activation(
-                    out=nbv[:, :, 64 * t : 64 * t + 64],
-                    in_=ch["s7"][:, q0 // QUAD, :, :],
-                    func=ACT.Copy,
-                    scale=ch["h"][:, q0 + ST, t : t + 1],
-                )
+        def log_sum(s):
+            la, lb, lt, n = logs[s]
+            l7s[s] = l7p.tile([P, 2, P], F32, tag="l7", name="l7")
+            return outer(
+                l7s[s][:].rearrange("p k (a b) -> p k a b", b=16), la[:, n : n + 2, :], lb[:, n : n + 2, :], ALU.add
+            )
 
         def quantise(sq):
             codes = cdp.tile([P, QUAD * P], U32, tag="codes", name="codes", align_bytes=64)
@@ -206,26 +249,62 @@ def tile_extendedanfis_t_kernel(tc, x, mfs, rules, out):
 
         def transposes(sq):
             nb = nbs[sq]
-            for half in range(2):
-                tp = tps.tile([P, 2, 2, P], F32, tag="tp", name="tp")
-                tpl[sq, half] = tp
+            for c in range(1 if sq in logs else 2):
+                tp = tps.tile([P, 4, P], F32, tag="tp", name="tp")
+                tpl[sq, c] = tp
                 for k in range(2):
                     for u in range(2):
-                        words = nb[:, half * 2 + k, 2 * P * u : 2 * P * (u + 1)].bitcast(F32)
-                        nc.tensor.transpose(tp[:, k, u, :], words, ident[:])
+                        words = nb[:, 2 * c + k, 2 * P * u : 2 * P * (u + 1)].bitcast(F32)
+                        nc.tensor.transpose(tp[:, 2 * k + u, :], words, ident[:])
+            if sq in logs:
+                la, lb, lt, n = logs[sq]
+                for k in range(2):
+                    tp = tps.tile([P, 4, P], F32, tag="tp", name="tp")
+                    tpl[sq, 2 + k] = tp
+                    for t in range(4):
+                        nc.tensor.matmul(
+                            tp[:, t, :], l7s[sq][:, k, :], ident[:], start=True, stop=False, is_transpose=True
+                        )
+                        nc.tensor.matmul(
+                            tp[:, t, :],
+                            lt[:, n + k, t : t + 1].to_broadcast([P, P]),
+                            ident[:],
+                            start=False,
+                            stop=True,
+                            is_transpose=True,
+                        )
 
-        def evacuate(sq, half, copy):
-            if half == 0:
-                gs[sq] = grp.tile([P, QUAD, P, 4], BF16, tag="g", name="g", align_bytes=64)
-            copy(
-                out=gs[sq][:, half * 2 : half * 2 + 2, :, :].bitcast(F32),
-                in_=tpl[sq, half][:].rearrange("p k u b -> p k b u"),
-            )
+        def evacuate(sq):
+            g = grp.tile([P, QUAD, P, 4], BF16, tag="g", name="g", align_bytes=64)
+            gs[sq] = g
+            for c in range(1 if sq in logs else 2):
+                nc.scalar.copy(
+                    out=g[:, 2 * c : 2 * c + 2, :, :].bitcast(F32),
+                    in_=tpl[sq, c][:].rearrange("p (k u) b -> p k b u", u=2),
+                )
+            if sq in logs:
+                for k in range(2):
+                    nc.scalar.activation(
+                        out=g[:, 2 + k, :, :],
+                        in_=tpl[sq, 2 + k][:].rearrange("p t b -> p b t"),
+                        func=ACT.Exp,
+                        scale=-0.5,
+                    )
 
         def multiply(sq, extra):
             codes, scales = cds[sq]
             po = ops.tile([P, QUAD, O], F32, tag="po", name="po")
             pos[sq] = po
+            for e in range(extra):
+                nc.tensor.matmul_mx(
+                    out=po[:].rearrange("p k o -> p (k o)"),
+                    lhsT=rcodes[:].bitcast(FP8X4),
+                    lhsT_scale=rscales[:],
+                    rhs=codes[:].bitcast(FP8X4),
+                    rhs_scale=scales[:],
+                    start=True,
+                    stop=True,
+                )
             for jj in range(QUAD):
                 nc.tensor.matmul_mx(
                     out=po[:, jj, :],
@@ -236,57 +315,74 @@ def tile_extendedanfis_t_kernel(tc, x, mfs, rules, out):
                     start=True,
                     stop=True,
                 )
-            for e in range(extra):
-                nc.tensor.matmul_mx(
-                    out=spare[:],
-                    lhsT=rcodes[:].bitcast(FP8X4),
-                    lhsT_scale=rscales[:],
-                    rhs=codes[:].bitcast(FP8X4),
-                    rhs_scale=scales[:],
-                    start=True,
-                    stop=True,
-                )
 
         def put_out(sq, copy):
             grp_i, pos_i = sq // GROUP, sq % GROUP
             if pos_i == 0:
                 osts[grp_i] = osp.tile([P, GROUP * QUAD, O], F32, tag="ost", name="ost")
             ost = osts[grp_i]
-            copy(out=ost[:, pos_i * QUAD : (pos_i + 1) * QUAD, :], in_=pos[sq][:])
+            rows = ost[:, pos_i * QUAD : (pos_i + 1) * QUAD, :]
+            copy(
+                out=rows.rearrange("p (w c) o -> p c w o", c=2),
+                in_=pos[sq][:].rearrange("p (c w) o -> p c w o", c=2),
+            )
             if grp_i == NQ // GROUP - 1:
-                nc.sync.dma_start(
-                    out=out_v[:, sq * QUAD : (sq + 1) * QUAD, :], in_=ost[:, pos_i * QUAD : (pos_i + 1) * QUAD, :]
-                )
+                nc.sync.dma_start(out=out_v[:, sq * QUAD : (sq + 1) * QUAD, :], in_=rows)
             elif pos_i == GROUP - 1:
                 nc.sync.dma_start(out=out_v[:, grp_i * GROUP * QUAD : (grp_i + 1) * GROUP * QUAD, :], in_=ost[:])
 
-        chunks[0] = make_chunk(0, CHUNKS[0])
-        for f in chunks[0]["sc"] + chunks[0]["rest"]:
+        v_more, s_more = {}, {}
+
+        def weave(table, s, fs):
+            table.setdefault(s, []).extend(fs)
+
+        m0 = memberships(small, "e", 0, EARLY[0])
+        for f in m0["squares"] + [m0["exps"](0, I)] + m0["chain"] + early_tables(m0, 0, EARLY[0]):
             f()
-        open_quad(0)
-        scalar_share(0)
-        pending = []
+        m1 = memberships(small, "e", EARLY[0], EARLY[1])
+        late = memberships(const, "late", NE, LATE)
+        lns = const.tile([P, LATE], F32)
+        warm = const.tile([P, 1], F32)
+        weave(s_more, 1, late["squares"])
+        weave(s_more, 1, [late["exps"](0, 4), late["exps"](4, I)])
+        weave(v_more, 2, late["chain"])
+        weave(
+            s_more,
+            2,
+            [
+                lambda: nc.scalar.activation(out=lns[:], in_=late["sum"][:], func=ACT.Ln),
+                lambda: nc.scalar.activation(out=warm[:], in_=lns[:, 0:1], func=ACT.Exp, scale=-0.5),
+            ],
+        )
+
+        next_sub = 0
+        sub_start = []
+        q = NE // QUAD
+        for w in SUBS:
+            sub_start.append(q)
+            q += w // QUAD
+
         for s in range(NQ + 4):
-            scalar_ops = []
             if s < NQ:
-                c, q0, n = quad_info[s]
-                extras = []
-                if q0 == 0 and c + 1 < len(CHUNKS):
-                    chunks[c + 1] = make_chunk(starts[c + 1], CHUNKS[c + 1])
-                    scalar_ops = chunks[c + 1]["sc"]
-                    pending = list(chunks[c + 1]["rest"])
-                if q0 > 0 and pending:
-                    left = max(1, n - 1 - q0 // QUAD)
-                    take = (len(pending) + left - 1) // left
-                    extras = pending[:take]
-                    pending = pending[take:]
-                if s == 0:
-                    for f in scalar_ops:
-                        f()
-                    scalar_ops = []
-                work = [direct(s, jj) for jj in range(QUAD) if jj != ST]
+                nbs[s] = nbp.tile([P, QUAD, 4 * P], BF16, tag="nb", name="nb", align_bytes=64)
+                if s == NE // QUAD - 1 or s in sub_start:
+                    if next_sub < len(SUBS):
+                        f, last = late_tables(
+                            late, lns, sub_start[next_sub], QUAD * sub_start[next_sub] - NE, SUBS[next_sub]
+                        )
+                        f = f + last
+                        span = max(1, sub_start[next_sub] - s)
+                        for k in range(span):
+                            weave(v_more, s + k, f[k * len(f) // span : (k + 1) * len(f) // span])
+                        next_sub += 1
+                work = [direct(s, 0)]
                 if s >= 2:
-                    work.insert(1, lambda: quantise(s - 2))
+                    work.append(lambda: quantise(s - 2))
+                work.append(log_sum(s) if s in logs else direct(s, 1))
+                extras = v_more.get(s, [])
+                if s == 0:
+                    for f in m1["squares"] + [m1["exps"](0, I)]:
+                        f()
                 done = 0
                 for k, f in enumerate(work):
                     f()
@@ -296,9 +392,8 @@ def tile_extendedanfis_t_kernel(tc, x, mfs, rules, out):
                     done = want
                 if s == 0:
                     nc.vector.tensor_copy(out=rg[:], in_=rl[:].rearrange("p t o -> p o t"))
-                    for f in pending:
+                    for f in m1["chain"] + early_tables(m1, 1, EARLY[1]):
                         f()
-                    pending = []
                     nc.vector.quantize_mx(
                         out=rcodes[:].bitcast(FP8X4), scales=rscales[:], in_=rg[:].rearrange("p o t -> p (o t)")
                     )
@@ -308,13 +403,9 @@ def tile_extendedanfis_t_kernel(tc, x, mfs, rules, out):
                 transposes(s - 1)
             if 3 <= s < NQ + 3:
                 multiply(s - 3, EXTRA if s < NQ else 0)
-            if s + 1 < NQ:
-                open_quad(s + 1)
-                scalar_share(s + 1)
             if s >= 4:
                 put_out(s - 4, nc.scalar.copy)
             if 1 <= s <= NQ:
-                for half in range(2):
-                    evacuate(s - 1, half, nc.scalar.copy)
-            for f in scalar_ops:
+                evacuate(s - 1)
+            for f in s_more.get(s, []):
                 f()

@@ -19,12 +19,11 @@ EPS = 1e-6
 FLOPS = 2 * B * R * O
 QUAD = 4
 NQ = NJ // QUAD
-EARLY = [4, 12]
-NE = sum(EARLY)
+NE = QUAD
 LATE = NJ - NE
-SUBS = [16, 32, 32, 32]
+SUBS = [12, 16, 32, 32, 32]
 GROUP = 4
-EXTRA = 1
+EXTRA = 0
 
 
 def tile_extendedanfis_t_kernel(tc, x, mfs, rules, out):
@@ -41,6 +40,11 @@ def tile_extendedanfis_t_kernel(tc, x, mfs, rules, out):
         ops = ctx.enter_context(tc.psum_pool(name="ops", bufs=2))
         ctx.enter_context(tc.manual_schedule())
 
+        ones = const.tile([P, 1], F32)
+        nc.vector.memset(ones[:], 1.0)
+        warm = const.tile([P, 1], F32)
+        nc.scalar.activation(out=warm[:], in_=ones[:], func=ACT.Exp)
+
         mf = const.tile([P, I * M * 2], BF16)
         nc.scalar.dma_start(out=mf[:], in_=mfs.rearrange("i m c -> (i m c)").partition_broadcast(P))
         xs = const.tile([P, NJ * I], BF16)
@@ -53,7 +57,9 @@ def tile_extendedanfis_t_kernel(tc, x, mfs, rules, out):
 
         mfv = mf[:].rearrange("p (k c) -> p k c", c=2)
         sg = const.tile([P, I * M], F32)
-        nc.scalar.activation(out=sg[:], in_=mfv[:, :, 1], func=ACT.Abs)
+        nc.vector.scalar_tensor_tensor(
+            out=sg[:], in0=mfv[:, :, 1], scalar=-1.0, in1=mfv[:, :, 1], op0=ALU.mult, op1=ALU.max
+        )
         nc.vector.tensor_scalar_add(out=sg[:], in0=sg[:], scalar1=EPS)
         rs = const.tile([P, I * M], F32)
         nc.vector.reciprocal(out=rs[:], in_=sg[:])
@@ -336,19 +342,16 @@ def tile_extendedanfis_t_kernel(tc, x, mfs, rules, out):
         def weave(table, s, fs):
             table.setdefault(s, []).extend(fs)
 
-        m0 = memberships(small, "e", 0, EARLY[0])
-        for f in m0["squares"] + [m0["exps"](0, I)] + m0["chain"] + early_tables(m0, 0, EARLY[0]):
-            f()
-        m1 = memberships(small, "e", EARLY[0], EARLY[1])
+        m0 = memberships(small, "e", 0, NE)
         late = memberships(const, "late", NE, LATE)
+        for f in m0["squares"] + [m0["exps"](0, I)] + m0["chain"] + early_tables(m0, 0, NE):
+            f()
+        for f in late["squares"] + [late["exps"](0, 4), late["exps"](4, I)]:
+            f()
         lns = const.tile([P, LATE], F32)
-        warm = const.tile([P, 1], F32)
-        weave(s_more, 1, late["squares"])
-        weave(s_more, 1, [late["exps"](0, 4), late["exps"](4, I)])
-        weave(v_more, 2, late["chain"])
         weave(
             s_more,
-            2,
+            0,
             [
                 lambda: nc.scalar.activation(out=lns[:], in_=late["sum"][:], func=ACT.Ln),
                 lambda: nc.scalar.activation(out=warm[:], in_=lns[:, 0:1], func=ACT.Exp, scale=-0.5),
@@ -365,24 +368,23 @@ def tile_extendedanfis_t_kernel(tc, x, mfs, rules, out):
         for s in range(NQ + 4):
             if s < NQ:
                 nbs[s] = nbp.tile([P, QUAD, 4 * P], BF16, tag="nb", name="nb", align_bytes=64)
-                if s == NE // QUAD - 1 or s in sub_start:
+                first_tables = []
+                if s == 0 or s in sub_start:
                     if next_sub < len(SUBS):
                         f, last = late_tables(
                             late, lns, sub_start[next_sub], QUAD * sub_start[next_sub] - NE, SUBS[next_sub]
                         )
+                        if s == 0:
+                            first_tables, f, last = f, last, []
                         f = f + last
                         span = max(1, sub_start[next_sub] - s)
                         for k in range(span):
-                            weave(v_more, s + k, f[k * len(f) // span : (k + 1) * len(f) // span])
+                            weave(v_more, max(s + k, 1), f[k * len(f) // span : (k + 1) * len(f) // span])
                         next_sub += 1
-                work = [direct(s, 0)]
+                work = [direct(s, 0), log_sum(s) if s in logs else direct(s, 1)]
                 if s >= 2:
                     work.append(lambda: quantise(s - 2))
-                work.append(log_sum(s) if s in logs else direct(s, 1))
                 extras = v_more.get(s, [])
-                if s == 0:
-                    for f in m1["squares"] + [m1["exps"](0, I)]:
-                        f()
                 done = 0
                 for k, f in enumerate(work):
                     f()
@@ -392,7 +394,7 @@ def tile_extendedanfis_t_kernel(tc, x, mfs, rules, out):
                     done = want
                 if s == 0:
                     nc.vector.tensor_copy(out=rg[:], in_=rl[:].rearrange("p t o -> p o t"))
-                    for f in m1["chain"] + early_tables(m1, 1, EARLY[1]):
+                    for f in late["chain"] + first_tables:
                         f()
                     nc.vector.quantize_mx(
                         out=rcodes[:].bitcast(FP8X4), scales=rscales[:], in_=rg[:].rearrange("p o t -> p (o t)")

@@ -19,11 +19,9 @@ EPS = 1e-6
 FLOPS = 2 * B * R * O
 QUAD = 4
 NQ = NJ // QUAD
-NE = QUAD
-LATE = NJ - NE
-SUBS = [12, 16, 32, 32, 32]
+SUBS = [16, 16, 32, 64]
+ON_VECTOR = 3
 GROUP = 4
-EXTRA = 0
 
 
 def tile_extendedanfis_t_kernel(tc, x, mfs, rules, out):
@@ -46,7 +44,7 @@ def tile_extendedanfis_t_kernel(tc, x, mfs, rules, out):
         nc.scalar.activation(out=warm[:], in_=ones[:], func=ACT.Exp)
 
         mf = const.tile([P, I * M * 2], BF16)
-        nc.scalar.dma_start(out=mf[:], in_=mfs.rearrange("i m c -> (i m c)").partition_broadcast(P))
+        nc.sync.dma_start(out=mf[:], in_=mfs.rearrange("i m c -> (i m c)").partition_broadcast(P))
         xs = const.tile([P, NJ * I], BF16)
         nc.sync.dma_start(out=xs[:], in_=x.rearrange("(p j) i -> p (j i)", j=NJ))
         rl = const.tile([P, 4, O], BF16)
@@ -90,54 +88,55 @@ def tile_extendedanfis_t_kernel(tc, x, mfs, rules, out):
         def flat(t):
             return t[:].rearrange("p j a b -> p j (a b)")
 
-        def memberships(pool, pre, j0, cj):
-            z = pool.tile([P, I, M, cj], F32, tag=pre + "z", name=pre + "z")
-            mb = pool.tile([P, I, M, cj], F32, tag=pre + "mb", name=pre + "mb")
-            s = pool.tile([P, I, cj], F32, tag=pre + "s", name=pre + "s")
-            t4 = pool.tile([P, 4, cj], F32, tag=pre + "t4", name=pre + "t4")
-            t2 = pool.tile([P, 2, cj], F32, tag=pre + "t2", name=pre + "t2")
-            t1 = pool.tile([P, cj], F32, tag=pre + "t1", name=pre + "t1")
-            rinv = pool.tile([P, cj], F32, tag=pre + "rinv", name=pre + "rinv")
-            xv = xs[:, j0 * I : (j0 + cj) * I].rearrange("p (j i) -> p j i", i=I)
+        z = const.tile([P, I, M, NJ], F32)
+        mb = const.tile([P, I, M, NJ], F32)
+        sums = const.tile([P, I, NJ], F32)
+        t4 = const.tile([P, 2, 2, NJ], F32)
+        t2 = const.tile([P, 2, NJ], F32)
+        t1 = const.tile([P, NJ], F32)
+        lns = const.tile([P, NJ], F32)
+        xv = xs[:].rearrange("p (j i) -> p i j", i=I)
 
-            def square(i, m):
+        def squares(i0, i1):
+            for i in range(i0, i1):
+                for m in range(M):
+                    k = i * M + m
+                    nc.scalar.activation(
+                        out=z[:, i, m, :],
+                        in_=xv[:, i, :],
+                        func=ACT.Square,
+                        scale=rs[:, k : k + 1],
+                        bias=bs[:, k : k + 1],
+                    )
+
+        def exponentials(i0, i1):
+            nc.scalar.activation(
+                out=mb[:, i0:i1, :, :].rearrange("p i m j -> p (i m j)"),
+                in_=z[:, i0:i1, :, :].rearrange("p i m j -> p (i m j)"),
+                func=ACT.Exp,
+                scale=-0.5,
+            )
+
+        zv = const.tile([P, ON_VECTOR, M, NJ], F32)
+        for i in range(I - ON_VECTOR, I):
+            for m in range(M):
                 k = i * M + m
-                return lambda: nc.scalar.activation(
-                    out=z[:, i, m, :],
-                    in_=xv[:, :, i],
-                    func=ACT.Square,
-                    scale=rs[:, k : k + 1],
-                    bias=bs[:, k : k + 1],
+                nc.vector.tensor_scalar(
+                    out=zv[:, i - (I - ON_VECTOR), m, :],
+                    in0=xv[:, i, :],
+                    scalar1=rs[:, k : k + 1],
+                    scalar2=bs[:, k : k + 1],
+                    op0=ALU.mult,
+                    op1=ALU.add,
                 )
+        nc.vector.tensor_tensor(out=z[:, I - ON_VECTOR : I, :, :], in0=zv[:], in1=zv[:], op=ALU.mult)
+        squares(0, I - ON_VECTOR)
+        exponentials(0, 4)
+        exponentials(4, 8)
+        exponentials(8, I)
 
-            def exps(i0, i1):
-                return lambda: nc.scalar.activation(
-                    out=mb[:, i0:i1, :, :].rearrange("p i m j -> p (i m j)"),
-                    in_=z[:, i0:i1, :, :].rearrange("p i m j -> p (i m j)"),
-                    func=ACT.Exp,
-                    scale=-0.5,
-                )
-
-            chain = [
-                tt(s[:], mb[:, :, 0, :], mb[:, :, 1, :], ALU.add),
-                tt(t4[:], s[:, 0:4, :], s[:, 4:8, :], ALU.mult),
-                tt(t2[:], t4[:, 0:2, :], t4[:, 2:4, :], ALU.mult),
-                tt(t1[:], t2[:, 0, :], t2[:, 1, :], ALU.mult),
-                tt(t1[:], t1[:], s[:, 8, :], ALU.mult),
-                lambda: nc.vector.tensor_scalar_add(out=t1[:], in0=t1[:], scalar1=EPS),
-                lambda: nc.vector.reciprocal(out=rinv[:], in_=t1[:]),
-            ]
-            return {
-                "squares": [square(i, m) for i in range(I) for m in range(M)],
-                "exps": exps,
-                "chain": chain,
-                "z": z,
-                "mb": mb,
-                "sum": t1,
-                "rinv": rinv,
-            }
-
-        def product_tables(pre, n, mem, rinv):
+        def product_tables(pre, n, mem, den):
+            rinv = small.tile([P, n], F32, tag=pre + "rinv", name=pre + "rinv")
             h0 = small.tile([P, n, 2, 2], F32, tag=pre + "h0", name=pre + "h0")
             h = small.tile([P, n, 4], F32, tag=pre + "h", name=pre + "h")
             hx = small.tile([P, n, 2, 4], F32, tag=pre + "hx", name=pre + "hx")
@@ -150,15 +149,16 @@ def tile_extendedanfis_t_kernel(tc, x, mfs, rules, out):
                 outer(h0[:], mem(0), mem(1)),
                 outer(c23[:], mem(2), mem(3)),
                 outer(c45[:], mem(4), mem(5)),
-                tt(h[:], flat(h0), rinv.unsqueeze(2).to_broadcast([P, n, 4]), ALU.mult),
                 outer(c68[:], mem(6), mem(8)),
-                outer(hx[:], mem(7), h[:]),
                 outer(yt[:], flat(c45), flat(c68)),
+                lambda: nc.vector.reciprocal(out=rinv[:], in_=den),
+                tt(h[:], flat(h0), rinv[:].unsqueeze(2).to_broadcast([P, n, 4]), ALU.mult),
+                outer(hx[:], mem(7), h[:]),
                 outer(xt[:], flat(hx), flat(c23)),
             ]
             return ops_, flat(xt), flat(yt)
 
-        def log_tables(pre, n, sq, lns):
+        def log_tables(pre, n, sq, lns_):
             l01 = small.tile([P, n, 2, 2], F32, tag=pre + "l01", name=pre + "l01")
             la = small.tile([P, n, 4, 2], F32, tag=pre + "la", name=pre + "la")
             l34 = small.tile([P, n, 2, 2], F32, tag=pre + "l34", name=pre + "l34")
@@ -177,7 +177,7 @@ def tile_extendedanfis_t_kernel(tc, x, mfs, rules, out):
             last = [
                 lambda: nc.vector.scalar_tensor_tensor(
                     out=lt[:],
-                    in0=lns.unsqueeze(2).to_broadcast([P, n, 4]),
+                    in0=lns_.unsqueeze(2).to_broadcast([P, n, 4]),
                     scalar=2.0,
                     in1=flat(l78),
                     op0=ALU.mult,
@@ -191,46 +191,30 @@ def tile_extendedanfis_t_kernel(tc, x, mfs, rules, out):
 
         nbs, l7s, gs, cds, pos, osts, tpl = {}, {}, {}, {}, {}, {}, {}
         prod, logs = {}, {}
+        sub_start = [sum(SUBS[:k]) // QUAD for k in range(len(SUBS))]
 
-        def early_tables(mem_chunk, s0, cj):
-            ops_ = []
-            for c in range(2):
-                o, xt, yt = product_tables(
-                    "e%d" % c,
-                    cj // 2,
-                    lambda i, c=c: pick(mem_chunk["mb"], i, 0, cj // 2, c),
-                    mem_chunk["rinv"][:].rearrange("p (n c) -> p c n", c=2)[:, c, :],
-                )
-                ops_.append(o)
-                for q in range(cj // QUAD):
-                    prod[s0 + q, c] = (xt, yt, 2 * q)
-            return [f for pair in zip(ops_[0], ops_[1]) for f in pair]
-
-        def late_tables(mem_chunk, lns, s0, j0, cj):
-            n = cj // 2
-            po, xt, yt = product_tables(
-                "l",
-                n,
-                lambda i: pick(mem_chunk["mb"], i, j0, n, 0),
-                mem_chunk["rinv"][:, j0 : j0 + cj].rearrange("p (n c) -> p c n", c=2)[:, 0, :],
+        def tables_of(k):
+            j0, n = QUAD * sub_start[k], SUBS[k] // 2
+            pr, xt, yt = product_tables(
+                "a", n, lambda i: pick(mb, i, j0, n, 0), t1[:, j0 : j0 + 2 * n].rearrange("p (n c) -> p c n", c=2)[:, 0, :]
             )
             lo, last, la, lb, lt = log_tables(
-                "l",
-                n,
-                lambda i: pick(mem_chunk["z"], i, j0, n, 1),
-                lns[:, j0 : j0 + cj].rearrange("p (n c) -> p c n", c=2)[:, 1, :],
+                "b", n, lambda i: pick(z, i, j0, n, 1), lns[:, j0 : j0 + 2 * n].rearrange("p (n c) -> p c n", c=2)[:, 1, :]
             )
-            for q in range(cj // QUAD):
-                prod[s0 + q, 0] = (xt, yt, 2 * q)
-                logs[s0 + q] = (la, lb, lt, 2 * q)
-            return [f for pair in zip(po, lo) for f in pair] + po[len(lo) :], last
+            for q in range(SUBS[k] // QUAD):
+                if sub_start[k] + q == NQ - 1:
+                    break
+                prod[sub_start[k] + q] = (xt, yt, 2 * q)
+                logs[sub_start[k] + q] = (la, lb, lt, 2 * q)
+            return lo, pr, last
 
-        def direct(s, c):
-            xt, yt, n = prod[s, c]
+        def direct(u, c=0):
+            xt, yt, n = prod[u]
+            n += 2 * c
 
             def go():
                 nc.vector.tensor_tensor(
-                    out=nbs[s][:, 2 * c : 2 * c + 2, :].rearrange("p k (a b) -> p k a b", b=16),
+                    out=nbs[u][:, 2 * c : 2 * c + 2, :].rearrange("p k (a b) -> p k a b", b=16),
                     in0=xt[:, n : n + 2, :].unsqueeze(3).to_broadcast([P, 2, 32, 16]),
                     in1=yt[:, n : n + 2, :].unsqueeze(2).to_broadcast([P, 2, 32, 16]),
                     op=ALU.mult,
@@ -238,80 +222,69 @@ def tile_extendedanfis_t_kernel(tc, x, mfs, rules, out):
 
             return go
 
-        def log_sum(s):
-            la, lb, lt, n = logs[s]
-            l7s[s] = l7p.tile([P, 2, P], F32, tag="l7", name="l7")
+        def log_sum(u):
+            la, lb, lt, n = logs[u]
+            l7s[u] = l7p.tile([P, 2, P], F32, tag="l7", name="l7")
             return outer(
-                l7s[s][:].rearrange("p k (a b) -> p k a b", b=16), la[:, n : n + 2, :], lb[:, n : n + 2, :], ALU.add
+                l7s[u][:].rearrange("p k (a b) -> p k a b", b=16), la[:, n : n + 2, :], lb[:, n : n + 2, :], ALU.add
             )
 
-        def quantise(sq):
-            codes = cdp.tile([P, QUAD * P], U32, tag="codes", name="codes", align_bytes=64)
-            scales = cdp.tile([P, QUAD * P], U8, tag="scales", name="scales", align_bytes=64)
-            cds[sq] = (codes, scales)
+        def quantise(u, c=0, parts=1):
+            w = QUAD * P // parts
+            codes = cdp.tile([P, w], U32, tag="codes", name="codes", align_bytes=64)
+            scales = cdp.tile([P, w], U8, tag="scales", name="scales", align_bytes=64)
+            cds[u, c] = (codes, scales)
             nc.vector.quantize_mx(
-                out=codes[:].bitcast(FP8X4), scales=scales[:], in_=gs[sq][:].rearrange("p k b t -> p (k b t)")
+                out=codes[:].bitcast(FP8X4), scales=scales[:], in_=gs[u][:].rearrange("p k b t -> p (k b t)")[:, 4 * w * c : 4 * w * (c + 1)]
             )
 
-        def transposes(sq):
-            nb = nbs[sq]
-            for c in range(1 if sq in logs else 2):
+        def transposes(u):
+            for c in range(2 if u == NQ - 1 else 1):
                 tp = tps.tile([P, 4, P], F32, tag="tp", name="tp")
-                tpl[sq, c] = tp
+                tpl[u, c] = tp
                 for k in range(2):
-                    for u in range(2):
-                        words = nb[:, 2 * c + k, 2 * P * u : 2 * P * (u + 1)].bitcast(F32)
-                        nc.tensor.transpose(tp[:, 2 * k + u, :], words, ident[:])
-            if sq in logs:
-                la, lb, lt, n = logs[sq]
-                for k in range(2):
-                    tp = tps.tile([P, 4, P], F32, tag="tp", name="tp")
-                    tpl[sq, 2 + k] = tp
-                    for t in range(4):
-                        nc.tensor.matmul(
-                            tp[:, t, :], l7s[sq][:, k, :], ident[:], start=True, stop=False, is_transpose=True
-                        )
-                        nc.tensor.matmul(
-                            tp[:, t, :],
-                            lt[:, n + k, t : t + 1].to_broadcast([P, P]),
-                            ident[:],
-                            start=False,
-                            stop=True,
-                            is_transpose=True,
-                        )
-
-        def evacuate(sq):
-            g = grp.tile([P, QUAD, P, 4], BF16, tag="g", name="g", align_bytes=64)
-            gs[sq] = g
-            for c in range(1 if sq in logs else 2):
-                nc.scalar.copy(
-                    out=g[:, 2 * c : 2 * c + 2, :, :].bitcast(F32),
-                    in_=tpl[sq, c][:].rearrange("p (k u) b -> p k b u", u=2),
-                )
-            if sq in logs:
-                for k in range(2):
-                    nc.scalar.activation(
-                        out=g[:, 2 + k, :, :],
-                        in_=tpl[sq, 2 + k][:].rearrange("p t b -> p b t"),
-                        func=ACT.Exp,
-                        scale=-0.5,
+                    for h in range(2):
+                        words = nbs[u][:, 2 * c + k, 2 * P * h : 2 * P * (h + 1)].bitcast(F32)
+                        nc.tensor.transpose(tp[:, 2 * k + h, :], words, ident[:])
+            if u == NQ - 1:
+                return
+            la, lb, lt, n = logs[u]
+            for k in range(2):
+                tp = tps.tile([P, 4, P], F32, tag="tp", name="tp")
+                tpl[u, 1 + k] = tp
+                for t in range(4):
+                    nc.tensor.matmul(tp[:, t, :], l7s[u][:, k, :], ident[:], start=True, stop=False, is_transpose=True)
+                    nc.tensor.matmul(
+                        tp[:, t, :],
+                        lt[:, n + k, t : t + 1].to_broadcast([P, P]),
+                        ident[:],
+                        start=False,
+                        stop=True,
+                        is_transpose=True,
                     )
 
-        def multiply(sq, extra):
-            codes, scales = cds[sq]
-            po = ops.tile([P, QUAD, O], F32, tag="po", name="po")
-            pos[sq] = po
-            for e in range(extra):
-                nc.tensor.matmul_mx(
-                    out=po[:].rearrange("p k o -> p (k o)"),
-                    lhsT=rcodes[:].bitcast(FP8X4),
-                    lhsT_scale=rscales[:],
-                    rhs=codes[:].bitcast(FP8X4),
-                    rhs_scale=scales[:],
-                    start=True,
-                    stop=True,
+        def evacuate_words(u, c, copy):
+            if c == 0:
+                gs[u] = grp.tile([P, QUAD, P, 4], BF16, tag="g", name="g", align_bytes=64)
+            copy(
+                out=gs[u][:, 2 * c : 2 * c + 2, :, :].bitcast(F32),
+                in_=tpl[u, c][:].rearrange("p (k h) b -> p k b h", h=2),
+            )
+
+        def evacuate_logs(u):
+            for k in range(2):
+                nc.scalar.activation(
+                    out=gs[u][:, 2 + k, :, :],
+                    in_=tpl[u, 1 + k][:].rearrange("p t b -> p b t"),
+                    func=ACT.Exp,
+                    scale=-0.5,
                 )
-            for jj in range(QUAD):
+
+        def multiply(u, c=0, parts=1):
+            codes, scales = cds[u, c]
+            po = ops.tile([P, QUAD, O], F32, tag="po", name="po")
+            pos[u, c] = po
+            for jj in range(QUAD // parts):
                 nc.tensor.matmul_mx(
                     out=po[:, jj, :],
                     lhsT=codes[:, jj * P : (jj + 1) * P].bitcast(FP8X4),
@@ -322,6 +295,9 @@ def tile_extendedanfis_t_kernel(tc, x, mfs, rules, out):
                     stop=True,
                 )
 
+        def store(j0, j1, rows):
+            nc.sync.dma_start(out=out_v[:, j0:j1, :], in_=rows)
+
         def put_out(sq, copy):
             grp_i, pos_i = sq // GROUP, sq % GROUP
             if pos_i == 0:
@@ -330,84 +306,93 @@ def tile_extendedanfis_t_kernel(tc, x, mfs, rules, out):
             rows = ost[:, pos_i * QUAD : (pos_i + 1) * QUAD, :]
             copy(
                 out=rows.rearrange("p (w c) o -> p c w o", c=2),
-                in_=pos[sq][:].rearrange("p (c w) o -> p c w o", c=2),
+                in_=pos[sq, 0][:].rearrange("p (c w) o -> p c w o", c=2),
             )
             if grp_i == NQ // GROUP - 1:
-                nc.sync.dma_start(out=out_v[:, sq * QUAD : (sq + 1) * QUAD, :], in_=rows)
+                store(sq * QUAD, (sq + 1) * QUAD, rows)
             elif pos_i == GROUP - 1:
-                nc.sync.dma_start(out=out_v[:, grp_i * GROUP * QUAD : (grp_i + 1) * GROUP * QUAD, :], in_=ost[:])
+                store(grp_i * GROUP * QUAD, (grp_i + 1) * GROUP * QUAD, ost[:])
 
-        v_more, s_more = {}, {}
+        def put_out_last(c, copy):
+            rows = osts[NQ // GROUP - 1][:, (GROUP - 1) * QUAD + 2 * c : (GROUP - 1) * QUAD + 2 * c + 2, :]
+            copy(out=rows, in_=pos[NQ - 1, c][:, 0:2, :])
+            store(NJ - QUAD + 2 * c, NJ - QUAD + 2 * c + 2, rows)
 
-        def weave(table, s, fs):
-            table.setdefault(s, []).extend(fs)
+        def sum_pair(i0, i1):
+            return tt(sums[:, i0:i1, :], mb[:, i0:i1, 0, :], mb[:, i0:i1, 1, :], ALU.add)
 
-        m0 = memberships(small, "e", 0, NE)
-        late = memberships(const, "late", NE, LATE)
-        for f in m0["squares"] + [m0["exps"](0, I)] + m0["chain"] + early_tables(m0, 0, NE):
+        def four(c):
+            return [
+                tt(t4[:, c, :, :], sums[:, 4 * c : 4 * c + 2, :], sums[:, 4 * c + 2 : 4 * c + 4, :], ALU.mult),
+                tt(t2[:, c, :], t4[:, c, 0, :], t4[:, c, 1, :], ALU.mult),
+            ]
+
+        lo, pr, pending = tables_of(0)
+        nc.vector.tensor_copy(out=rg[:], in_=rl[:].rearrange("p t o -> p o t"))
+        head = lo + [sum_pair(0, 4)] + pr[:1] + four(0)[:1] + pr[1:2] + four(0)[1:]
+        head += [sum_pair(4, 8)] + pr[2:3] + four(1)[:1] + [sum_pair(8, I)] + four(1)[1:] + pr[3:4]
+        head += [
+            tt(t1[:], t2[:, 0, :], sums[:, 8, :], ALU.mult),
+            pr[4],
+            tt(t1[:], t1[:], t2[:, 1, :], ALU.mult),
+            lambda: nc.vector.tensor_scalar_add(out=t1[:], in0=t1[:], scalar1=EPS),
+        ]
+        for f in head + pr[5:]:
             f()
-        for f in late["squares"] + [late["exps"](0, 4), late["exps"](4, I)]:
-            f()
-        lns = const.tile([P, LATE], F32)
-        weave(
-            s_more,
-            0,
-            [
-                lambda: nc.scalar.activation(out=lns[:], in_=late["sum"][:], func=ACT.Ln),
-                lambda: nc.scalar.activation(out=warm[:], in_=lns[:, 0:1], func=ACT.Exp, scale=-0.5),
-            ],
+        nc.scalar.activation(out=lns[:], in_=t1[:], func=ACT.Ln)
+        nc.scalar.activation(out=warm[:], in_=lns[:, 0:1], func=ACT.Exp, scale=-0.5)
+
+        nc.vector.quantize_mx(
+            out=rcodes[:].bitcast(FP8X4), scales=rscales[:], in_=rg[:].rearrange("p o t -> p (o t)")
         )
-
-        next_sub = 0
-        sub_start = []
-        q = NE // QUAD
-        for w in SUBS:
-            sub_start.append(q)
-            q += w // QUAD
-
-        for s in range(NQ + 4):
-            if s < NQ:
-                nbs[s] = nbp.tile([P, QUAD, 4 * P], BF16, tag="nb", name="nb", align_bytes=64)
-                first_tables = []
-                if s == 0 or s in sub_start:
-                    if next_sub < len(SUBS):
-                        f, last = late_tables(
-                            late, lns, sub_start[next_sub], QUAD * sub_start[next_sub] - NE, SUBS[next_sub]
-                        )
-                        if s == 0:
-                            first_tables, f, last = f, last, []
-                        f = f + last
-                        span = max(1, sub_start[next_sub] - s)
-                        for k in range(span):
-                            weave(v_more, max(s + k, 1), f[k * len(f) // span : (k + 1) * len(f) // span])
-                        next_sub += 1
-                work = [direct(s, 0), log_sum(s) if s in logs else direct(s, 1)]
-                if s >= 2:
-                    work.append(lambda: quantise(s - 2))
-                extras = v_more.get(s, [])
-                done = 0
-                for k, f in enumerate(work):
-                    f()
-                    want = (k + 1) * len(extras) // len(work)
-                    for e in extras[done:want]:
-                        e()
-                    done = want
-                if s == 0:
-                    nc.vector.tensor_copy(out=rg[:], in_=rl[:].rearrange("p t o -> p o t"))
-                    for f in late["chain"] + first_tables:
-                        f()
-                    nc.vector.quantize_mx(
-                        out=rcodes[:].bitcast(FP8X4), scales=rscales[:], in_=rg[:].rearrange("p o t -> p (o t)")
-                    )
-            elif s - 2 < NQ:
-                quantise(s - 2)
-            if 1 <= s <= NQ:
-                transposes(s - 1)
-            if 3 <= s < NQ + 3:
-                multiply(s - 3, EXTRA if s < NQ else 0)
-            if s >= 4:
-                put_out(s - 4, nc.scalar.copy)
-            if 1 <= s <= NQ:
-                evacuate(s - 1)
-            for f in s_more.get(s, []):
+        for u in range(NQ):
+            nbs[u] = nbp.tile([P, QUAD if u == NQ - 1 else 2, 4 * P], BF16, tag="nb", name="nb", align_bytes=64)
+            k = [k for k in range(len(SUBS)) if sub_start[k] <= u][-1]
+            if u == sub_start[k] and k + 1 < len(SUBS):
+                lo, pr, more = tables_of(k + 1)
+                pending = pending + [f for pair in zip(pr, lo + more) for f in pair] + pr[len(lo + more) :]
+            if u == 1:
+                last_tables, xt, yt = product_tables(
+                    "z", QUAD, lambda i: mb[:, i, :, NJ - QUAD : NJ].rearrange("p m j -> p j m"), t1[:, NJ - QUAD : NJ]
+                )
+                prod[NQ - 1] = (xt, yt, 0)
+            left = [v for v in range(u, NQ) if k + 1 == len(SUBS) or v < sub_start[k + 1]]
+            take = (len(pending) + len(left) - 1) // len(left)
+            extras, pending = pending[:take], pending[take:]
+            if u == 1:
+                extras = extras + last_tables
+            work = [direct(u), direct(u, 1) if u == NQ - 1 else log_sum(u)]
+            if u >= 2:
+                work.append(lambda: quantise(u - 2))
+            done = 0
+            for i, f in enumerate(work):
                 f()
+                want = (i + 1) * len(extras) // len(work)
+                for e in extras[done:want]:
+                    e()
+                done = want
+            if u >= 1:
+                transposes(u - 1)
+            if u >= 3:
+                multiply(u - 3)
+            if u >= 4:
+                put_out(u - 4, nc.scalar.copy)
+            if u >= 1:
+                evacuate_words(u - 1, 0, nc.scalar.copy)
+                evacuate_logs(u - 1)
+
+        transposes(NQ - 1)
+        put_out(NQ - 4, nc.vector.tensor_copy)
+        multiply(NQ - 3)
+        quantise(NQ - 2)
+        evacuate_words(NQ - 1, 0, nc.vector.tensor_copy)
+        evacuate_words(NQ - 1, 1, nc.scalar.copy)
+        quantise(NQ - 1, 0, 2)
+        quantise(NQ - 1, 1, 2)
+        put_out(NQ - 3, nc.scalar.copy)
+        multiply(NQ - 2)
+        put_out(NQ - 2, nc.vector.tensor_copy)
+        multiply(NQ - 1, 0, 2)
+        multiply(NQ - 1, 1, 2)
+        put_out_last(0, nc.scalar.copy)
+        put_out_last(1, nc.vector.tensor_copy)

@@ -19,8 +19,11 @@ EPS = 1e-6
 FLOPS = 2 * B * R * O
 QUAD = 4
 NQ = NJ // QUAD
-SUBS = [16, 16, 32, 64]
+UNITS = [1, 1] + [2] * 14 + [1, 1]
+NU = len(UNITS)
+SUBS = [16, 24, 32, 56]
 ON_VECTOR = 3
+WIDE = 4
 GROUP = 4
 
 
@@ -154,8 +157,9 @@ def tile_extendedanfis_t_kernel(tc, x, mfs, rules, out):
                 lambda: nc.vector.reciprocal(out=rinv[:], in_=den),
                 tt(h[:], flat(h0), rinv[:].unsqueeze(2).to_broadcast([P, n, 4]), ALU.mult),
                 outer(hx[:], mem(7), h[:]),
-                outer(xt[:], flat(hx), flat(c23)),
             ]
+            for n0, n1 in ((0, n // 2), (n // 2, n)):
+                ops_.append(outer(xt[:, n0:n1, :, :], flat(hx)[:, n0:n1, :], flat(c23)[:, n0:n1, :]))
             return ops_, flat(xt), flat(yt)
 
         def log_tables(pre, n, sq, lns_):
@@ -191,6 +195,7 @@ def tile_extendedanfis_t_kernel(tc, x, mfs, rules, out):
 
         nbs, l7s, gs, cds, pos, osts, tpl = {}, {}, {}, {}, {}, {}, {}
         prod, logs = {}, {}
+        first = [sum(UNITS[:u]) for u in range(NU)]
         sub_start = [sum(SUBS[:k]) // QUAD for k in range(len(SUBS))]
 
         def tables_of(k):
@@ -209,28 +214,30 @@ def tile_extendedanfis_t_kernel(tc, x, mfs, rules, out):
             return lo, pr, last
 
         def direct(u, c=0):
-            xt, yt, n = prod[u]
+            xt, yt, n = prod[first[u]]
+            w = 2 * UNITS[u]
             n += 2 * c
 
             def go():
                 nc.vector.tensor_tensor(
-                    out=nbs[u][:, 2 * c : 2 * c + 2, :].rearrange("p k (a b) -> p k a b", b=16),
-                    in0=xt[:, n : n + 2, :].unsqueeze(3).to_broadcast([P, 2, 32, 16]),
-                    in1=yt[:, n : n + 2, :].unsqueeze(2).to_broadcast([P, 2, 32, 16]),
+                    out=nbs[u][:, 2 * c : 2 * c + w, :].rearrange("p k (a b) -> p k a b", b=16),
+                    in0=xt[:, n : n + w, :].unsqueeze(3).to_broadcast([P, w, 32, 16]),
+                    in1=yt[:, n : n + w, :].unsqueeze(2).to_broadcast([P, w, 32, 16]),
                     op=ALU.mult,
                 )
 
             return go
 
         def log_sum(u):
-            la, lb, lt, n = logs[u]
-            l7s[u] = l7p.tile([P, 2, P], F32, tag="l7", name="l7")
+            la, lb, lt, n = logs[first[u]]
+            w = 2 * UNITS[u]
+            l7s[u] = l7p.tile([P, w, P], F32, tag="l7", name="l7")
             return outer(
-                l7s[u][:].rearrange("p k (a b) -> p k a b", b=16), la[:, n : n + 2, :], lb[:, n : n + 2, :], ALU.add
+                l7s[u][:].rearrange("p k (a b) -> p k a b", b=16), la[:, n : n + w, :], lb[:, n : n + w, :], ALU.add
             )
 
         def quantise(u, c=0, parts=1):
-            w = QUAD * P // parts
+            w = QUAD * UNITS[u] * P // parts
             codes = cdp.tile([P, w], U32, tag="codes", name="codes", align_bytes=64)
             scales = cdp.tile([P, w], U8, tag="scales", name="scales", align_bytes=64)
             cds[u, c] = (codes, scales)
@@ -238,20 +245,23 @@ def tile_extendedanfis_t_kernel(tc, x, mfs, rules, out):
                 out=codes[:].bitcast(FP8X4), scales=scales[:], in_=gs[u][:].rearrange("p k b t -> p (k b t)")[:, 4 * w * c : 4 * w * (c + 1)]
             )
 
+        def words(u):
+            return 2 if u == NU - 1 else UNITS[u]
+
         def transposes(u):
-            for c in range(2 if u == NQ - 1 else 1):
+            for c in range(words(u)):
                 tp = tps.tile([P, 4, P], F32, tag="tp", name="tp")
                 tpl[u, c] = tp
                 for k in range(2):
                     for h in range(2):
-                        words = nbs[u][:, 2 * c + k, 2 * P * h : 2 * P * (h + 1)].bitcast(F32)
-                        nc.tensor.transpose(tp[:, 2 * k + h, :], words, ident[:])
-            if u == NQ - 1:
+                        pairs = nbs[u][:, 2 * c + k, 2 * P * h : 2 * P * (h + 1)].bitcast(F32)
+                        nc.tensor.transpose(tp[:, 2 * k + h, :], pairs, ident[:])
+            if u == NU - 1:
                 return
-            la, lb, lt, n = logs[u]
-            for k in range(2):
+            la, lb, lt, n = logs[first[u]]
+            for k in range(2 * UNITS[u]):
                 tp = tps.tile([P, 4, P], F32, tag="tp", name="tp")
-                tpl[u, 1 + k] = tp
+                tpl[u, words(u) + k] = tp
                 for t in range(4):
                     nc.tensor.matmul(tp[:, t, :], l7s[u][:, k, :], ident[:], start=True, stop=False, is_transpose=True)
                     nc.tensor.matmul(
@@ -265,35 +275,39 @@ def tile_extendedanfis_t_kernel(tc, x, mfs, rules, out):
 
         def evacuate_words(u, c, copy):
             if c == 0:
-                gs[u] = grp.tile([P, QUAD, P, 4], BF16, tag="g", name="g", align_bytes=64)
+                gs[u] = grp.tile([P, QUAD * UNITS[u], P, 4], BF16, tag="g", name="g", align_bytes=64)
             copy(
                 out=gs[u][:, 2 * c : 2 * c + 2, :, :].bitcast(F32),
                 in_=tpl[u, c][:].rearrange("p (k h) b -> p k b h", h=2),
             )
 
         def evacuate_logs(u):
-            for k in range(2):
+            for k in range(2 * UNITS[u]):
                 nc.scalar.activation(
-                    out=gs[u][:, 2 + k, :, :],
-                    in_=tpl[u, 1 + k][:].rearrange("p t b -> p b t"),
+                    out=gs[u][:, 2 * UNITS[u] + k, :, :],
+                    in_=tpl[u, words(u) + k][:].rearrange("p t b -> p b t"),
                     func=ACT.Exp,
                     scale=-0.5,
                 )
 
-        def multiply(u, c=0, parts=1):
+        def multiply(u, q, slots, c=0):
             codes, scales = cds[u, c]
             po = ops.tile([P, QUAD, O], F32, tag="po", name="po")
-            pos[u, c] = po
-            for jj in range(QUAD // parts):
+            pos[first[u] + q, c] = po
+            for jj, slot in enumerate(slots):
                 nc.tensor.matmul_mx(
                     out=po[:, jj, :],
-                    lhsT=codes[:, jj * P : (jj + 1) * P].bitcast(FP8X4),
-                    lhsT_scale=scales[:, jj * P : (jj + 1) * P],
+                    lhsT=codes[:, slot * P : (slot + 1) * P].bitcast(FP8X4),
+                    lhsT_scale=scales[:, slot * P : (slot + 1) * P],
                     rhs=rcodes[:].bitcast(FP8X4),
                     rhs_scale=rscales[:],
                     start=True,
                     stop=True,
                 )
+
+        def multiply_unit(u):
+            for q in range(UNITS[u]):
+                multiply(u, q, [2 * q, 2 * q + 1, 2 * (UNITS[u] + q), 2 * (UNITS[u] + q) + 1])
 
         def store(j0, j1, rows):
             nc.sync.dma_start(out=out_v[:, j0:j1, :], in_=rows)
@@ -327,7 +341,8 @@ def tile_extendedanfis_t_kernel(tc, x, mfs, rules, out):
                 tt(t2[:, c, :], t4[:, c, 0, :], t4[:, c, 1, :], ALU.mult),
             ]
 
-        lo, pr, pending = tables_of(0)
+        lo, pr, more = tables_of(0)
+        pending = [(f, 1) for f in more]
         nc.vector.tensor_copy(out=rg[:], in_=rl[:].rearrange("p t o -> p o t"))
         head = lo + [sum_pair(0, 4)] + pr[:1] + four(0)[:1] + pr[1:2] + four(0)[1:]
         head += [sum_pair(4, 8)] + pr[2:3] + four(1)[:1] + [sum_pair(8, I)] + four(1)[1:] + pr[3:4]
@@ -345,23 +360,30 @@ def tile_extendedanfis_t_kernel(tc, x, mfs, rules, out):
         nc.vector.quantize_mx(
             out=rcodes[:].bitcast(FP8X4), scales=rscales[:], in_=rg[:].rearrange("p o t -> p (o t)")
         )
-        for u in range(NQ):
-            nbs[u] = nbp.tile([P, QUAD if u == NQ - 1 else 2, 4 * P], BF16, tag="nb", name="nb", align_bytes=64)
-            k = [k for k in range(len(SUBS)) if sub_start[k] <= u][-1]
-            if u == sub_start[k] and k + 1 < len(SUBS):
+        for u in range(NU):
+            nbs[u] = nbp.tile(
+                [P, QUAD if u == NU - 1 else 2 * UNITS[u], 4 * P], BF16, tag="nb", name="nb", align_bytes=64
+            )
+            k = [k for k in range(len(SUBS)) if sub_start[k] <= first[u]][-1]
+            if first[u] == sub_start[k] and k + 1 < len(SUBS):
                 lo, pr, more = tables_of(k + 1)
-                pending = pending + [f for pair in zip(pr, lo + more) for f in pair] + pr[len(lo + more) :]
-            if u == 1:
+                order = pr[:5] + lo[:3] + pr[5:8] + lo[3:] + pr[8:9] + more + pr[9:]
+                pending = pending + [(f, WIDE if f in (pr[4], pr[8], pr[9], lo[5]) else 1) for f in order]
+            if u == 3:
                 last_tables, xt, yt = product_tables(
                     "z", QUAD, lambda i: mb[:, i, :, NJ - QUAD : NJ].rearrange("p m j -> p j m"), t1[:, NJ - QUAD : NJ]
                 )
                 prod[NQ - 1] = (xt, yt, 0)
-            left = [v for v in range(u, NQ) if k + 1 == len(SUBS) or v < sub_start[k + 1]]
-            take = (len(pending) + len(left) - 1) // len(left)
-            extras, pending = pending[:take], pending[take:]
-            if u == 1:
+            left = [v for v in range(u, NU) if k + 1 == len(SUBS) or first[v] < sub_start[k + 1]]
+            share = sum(w for f, w in pending) / len(left)
+            n_now, sum_now = 0, 0
+            for f, w in pending:
+                if sum_now < share:
+                    n_now, sum_now = n_now + 1, sum_now + w
+            extras, pending = [f for f, w in pending[:n_now]], pending[n_now:]
+            if u == 3:
                 extras = extras + last_tables
-            work = [direct(u), direct(u, 1) if u == NQ - 1 else log_sum(u)]
+            work = [direct(u), direct(u, 1) if u == NU - 1 else log_sum(u)]
             if u >= 2:
                 work.append(lambda: quantise(u - 2))
             done = 0
@@ -374,25 +396,29 @@ def tile_extendedanfis_t_kernel(tc, x, mfs, rules, out):
             if u >= 1:
                 transposes(u - 1)
             if u >= 3:
-                multiply(u - 3)
+                multiply_unit(u - 3)
             if u >= 4:
-                put_out(u - 4, nc.scalar.copy)
+                for q in range(UNITS[u - 4]):
+                    put_out(first[u - 4] + q, nc.scalar.copy)
             if u >= 1:
-                evacuate_words(u - 1, 0, nc.scalar.copy)
+                for c in range(words(u - 1)):
+                    evacuate_words(u - 1, c, nc.scalar.copy)
                 evacuate_logs(u - 1)
 
-        transposes(NQ - 1)
-        put_out(NQ - 4, nc.vector.tensor_copy)
-        multiply(NQ - 3)
-        quantise(NQ - 2)
-        evacuate_words(NQ - 1, 0, nc.vector.tensor_copy)
-        evacuate_words(NQ - 1, 1, nc.scalar.copy)
-        quantise(NQ - 1, 0, 2)
-        quantise(NQ - 1, 1, 2)
-        put_out(NQ - 3, nc.scalar.copy)
-        multiply(NQ - 2)
-        put_out(NQ - 2, nc.vector.tensor_copy)
-        multiply(NQ - 1, 0, 2)
-        multiply(NQ - 1, 1, 2)
-        put_out_last(0, nc.scalar.copy)
-        put_out_last(1, nc.vector.tensor_copy)
+        transposes(NU - 1)
+        put_out(NQ - 6, nc.vector.tensor_copy)
+        put_out(NQ - 5, nc.vector.tensor_copy)
+        multiply_unit(NU - 3)
+        quantise(NU - 2)
+        evacuate_words(NU - 1, 0, nc.vector.tensor_copy)
+        evacuate_words(NU - 1, 1, nc.scalar.copy)
+        quantise(NU - 1, 0, 2)
+        quantise(NU - 1, 1, 2)
+        put_out(NQ - 4, nc.scalar.copy)
+        multiply_unit(NU - 2)
+        put_out(NQ - 3, nc.vector.tensor_copy)
+        multiply(NU - 1, 0, [0, 1], 0)
+        put_out(NQ - 2, nc.scalar.copy)
+        multiply(NU - 1, 0, [0, 1], 1)
+        put_out_last(0, nc.vector.tensor_copy)
+        put_out_last(1, nc.scalar.copy)

@@ -23,6 +23,7 @@ UNITS = [1, 1] + [2] * 14 + [1, 1]
 NU = len(UNITS)
 SUBS = [16, 24, 32, 56]
 ON_VECTOR = 3
+EXTRA = 2
 WIDE = 4
 GROUP = 4
 
@@ -33,6 +34,7 @@ def tile_extendedanfis_t_kernel(tc, x, mfs, rules, out):
         const = ctx.enter_context(tc.tile_pool(name="const", bufs=1))
         small = ctx.enter_context(tc.tile_pool(name="small", bufs=2))
         l7p = ctx.enter_context(tc.tile_pool(name="l7p", bufs=3))
+        s7p = ctx.enter_context(tc.tile_pool(name="s7p", bufs=2))
         nbp = ctx.enter_context(tc.tile_pool(name="nbp", bufs=4))
         grp = ctx.enter_context(tc.tile_pool(name="grp", bufs=4))
         cdp = ctx.enter_context(tc.tile_pool(name="cdp", bufs=4))
@@ -142,11 +144,10 @@ def tile_extendedanfis_t_kernel(tc, x, mfs, rules, out):
             rinv = small.tile([P, n], F32, tag=pre + "rinv", name=pre + "rinv")
             h0 = small.tile([P, n, 2, 2], F32, tag=pre + "h0", name=pre + "h0")
             h = small.tile([P, n, 4], F32, tag=pre + "h", name=pre + "h")
-            hx = small.tile([P, n, 2, 4], F32, tag=pre + "hx", name=pre + "hx")
             c23 = small.tile([P, n, 2, 2], F32, tag=pre + "c23", name=pre + "c23")
             c45 = small.tile([P, n, 2, 2], F32, tag=pre + "c45", name=pre + "c45")
             c68 = small.tile([P, n, 2, 2], F32, tag=pre + "c68", name=pre + "c68")
-            xt = small.tile([P, n, 8, 4], F32, tag=pre + "xt", name=pre + "xt")
+            at = small.tile([P, n, 2, 4], F32, tag=pre + "at", name=pre + "at")
             yt = small.tile([P, n, 4, 4], F32, tag=pre + "yt", name=pre + "yt")
             ops_ = [
                 outer(h0[:], mem(0), mem(1)),
@@ -156,11 +157,9 @@ def tile_extendedanfis_t_kernel(tc, x, mfs, rules, out):
                 outer(yt[:], flat(c45), flat(c68)),
                 lambda: nc.vector.reciprocal(out=rinv[:], in_=den),
                 tt(h[:], flat(h0), rinv[:].unsqueeze(2).to_broadcast([P, n, 4]), ALU.mult),
-                outer(hx[:], mem(7), h[:]),
+                outer(at[:], mem(7), flat(c23)),
             ]
-            for n0, n1 in ((0, n // 2), (n // 2, n)):
-                ops_.append(outer(xt[:, n0:n1, :, :], flat(hx)[:, n0:n1, :], flat(c23)[:, n0:n1, :]))
-            return ops_, flat(xt), flat(yt)
+            return ops_, (flat(at), flat(yt), h)
 
         def log_tables(pre, n, sq, lns_):
             l01 = small.tile([P, n, 2, 2], F32, tag=pre + "l01", name=pre + "l01")
@@ -193,48 +192,72 @@ def tile_extendedanfis_t_kernel(tc, x, mfs, rules, out):
         def pick(t, i, j0, n, c):
             return t[:, i, :, j0 : j0 + 2 * n].rearrange("p m (n c) -> p c n m", c=2)[:, c, :, :]
 
-        nbs, l7s, gs, cds, pos, osts, tpl = {}, {}, {}, {}, {}, {}, {}
+        s7s, nbs, l7s, gs, cds, pos, osts, tpl = {}, {}, {}, {}, {}, {}, {}, {}
         prod, logs = {}, {}
+        on_vector = range(sum(SUBS[:-1]) // QUAD, NQ, 4)
         first = [sum(UNITS[:u]) for u in range(NU)]
+        extra = [u for u in range(4, NU) if first[u] % 4 == 2 and UNITS[u] == 2]
+
+        def products(u):
+            return QUAD if u == NU - 1 else 2 * UNITS[u] + (u in extra)
+
         sub_start = [sum(SUBS[:k]) // QUAD for k in range(len(SUBS))]
+
+        def odd(i):
+            return mb[:, i, :, :].rearrange("p m (n w) -> p w n m", w=16)[:, 13, :, :]
 
         def tables_of(k):
             j0, n = QUAD * sub_start[k], SUBS[k] // 2
-            pr, xt, yt = product_tables(
+            pr, factors = product_tables(
                 "a", n, lambda i: pick(mb, i, j0, n, 0), t1[:, j0 : j0 + 2 * n].rearrange("p (n c) -> p c n", c=2)[:, 0, :]
             )
             lo, last, la, lb, lt = log_tables(
                 "b", n, lambda i: pick(z, i, j0, n, 1), lns[:, j0 : j0 + 2 * n].rearrange("p (n c) -> p c n", c=2)[:, 1, :]
             )
-            for q in range(SUBS[k] // QUAD):
-                if sub_start[k] + q == NQ - 1:
-                    break
-                prod[sub_start[k] + q] = (xt, yt, 2 * q)
-                logs[sub_start[k] + q] = (la, lb, lt, 2 * q)
+            for u in range(NU - 1):
+                q = first[u] - sub_start[k]
+                if 0 <= q < SUBS[k] // QUAD:
+                    prod.setdefault(u, []).append((factors, 2 * q, 0, 2 * UNITS[u]))
+                    logs[first[u]] = (la, lb, lt, 2 * q)
             return lo, pr, last
 
-        def direct(u, c=0):
-            xt, yt, n = prod[first[u]]
-            w = 2 * UNITS[u]
-            n += 2 * c
-
-            def go():
-                nc.vector.tensor_tensor(
-                    out=nbs[u][:, 2 * c : 2 * c + w, :].rearrange("p k (a b) -> p k a b", b=16),
-                    in0=xt[:, n : n + w, :].unsqueeze(3).to_broadcast([P, w, 32, 16]),
-                    in1=yt[:, n : n + w, :].unsqueeze(2).to_broadcast([P, w, 32, 16]),
-                    op=ALU.mult,
+        def seven(u):
+            s7s[u] = s7p.tile([P, products(u), 2, 64], F32, tag="s7", name="s7")
+            ops_ = []
+            for (at, yt, h), n, s0, s1 in prod[u]:
+                ops_.append(
+                    outer(
+                        s7s[u][:, s0:s1, :, :].rearrange("p k e (a b) -> p k (e a) b", b=16),
+                        at[:, n : n + s1 - s0, :],
+                        yt[:, n : n + s1 - s0, :],
+                    )
                 )
+            return ops_
 
-            return go
+        def block(u, slot, c):
+            (at, yt, h), n, s0, s1 = [e for e in prod[u] if e[2] <= slot < e[3]][0]
+            n -= s0
+            return lambda: nc.vector.tensor_scalar(
+                out=nbs[u][:, slot, :].rearrange("p (e w) -> p e w", e=2)[:, :, 64 * c : 64 * c + 64],
+                in0=s7s[u][:, slot, :, :],
+                scalar1=h[:, n + slot, c : c + 1],
+                scalar2=None,
+                op0=ALU.mult,
+            )
 
         def log_sum(u):
             la, lb, lt, n = logs[first[u]]
-            w = 2 * UNITS[u]
-            l7s[u] = l7p.tile([P, w, P], F32, tag="l7", name="l7")
-            return outer(
-                l7s[u][:].rearrange("p k (a b) -> p k a b", b=16), la[:, n : n + w, :], lb[:, n : n + w, :], ALU.add
-            )
+            l7s[u] = l7p.tile([P, 2 * UNITS[u], P], F32, tag="l7", name="l7")
+            runs = [(0, EXTRA), (EXTRA + 1, 2 * UNITS[u])] if u in extra else [(0, 2 * UNITS[u])]
+            return [
+                outer(
+                    l7s[u][:, k0:k1, :].rearrange("p k (a b) -> p k a b", b=16),
+                    la[:, n + k0 : n + k1, :],
+                    lb[:, n + k0 : n + k1, :],
+                    ALU.add,
+                )
+                for k0, k1 in runs
+            ]
 
         def quantise(u, c=0, parts=1):
             w = QUAD * UNITS[u] * P // parts
@@ -248,6 +271,9 @@ def tile_extendedanfis_t_kernel(tc, x, mfs, rules, out):
         def words(u):
             return 2 if u == NU - 1 else UNITS[u]
 
+        def by_logs(u):
+            return [k for k in range(2 * UNITS[u]) if not (u in extra and k == EXTRA)]
+
         def transposes(u):
             for c in range(words(u)):
                 tp = tps.tile([P, 4, P], F32, tag="tp", name="tp")
@@ -258,8 +284,14 @@ def tile_extendedanfis_t_kernel(tc, x, mfs, rules, out):
                         nc.tensor.transpose(tp[:, 2 * k + h, :], pairs, ident[:])
             if u == NU - 1:
                 return
+            if u in extra:
+                tp = tps.tile([P, 4, P], F32, tag="tp", name="tp")
+                tpl[u, words(u) + EXTRA] = tp
+                for h in range(2):
+                    pairs = nbs[u][:, 2 * UNITS[u], 2 * P * h : 2 * P * (h + 1)].bitcast(F32)
+                    nc.tensor.transpose(tp[:, h, :], pairs, ident[:])
             la, lb, lt, n = logs[first[u]]
-            for k in range(2 * UNITS[u]):
+            for k in by_logs(u):
                 tp = tps.tile([P, 4, P], F32, tag="tp", name="tp")
                 tpl[u, words(u) + k] = tp
                 for t in range(4):
@@ -282,7 +314,13 @@ def tile_extendedanfis_t_kernel(tc, x, mfs, rules, out):
             )
 
         def evacuate_logs(u):
-            for k in range(2 * UNITS[u]):
+            if u in extra:
+                slot = 2 * UNITS[u] + EXTRA
+                nc.scalar.copy(
+                    out=gs[u][:, slot, :, :].bitcast(F32),
+                    in_=tpl[u, words(u) + EXTRA][:, 0:2, :].rearrange("p h b -> p b h"),
+                )
+            for k in by_logs(u):
                 nc.scalar.activation(
                     out=gs[u][:, 2 * UNITS[u] + k, :, :],
                     in_=tpl[u, words(u) + k][:].rearrange("p t b -> p b t"),
@@ -361,31 +399,38 @@ def tile_extendedanfis_t_kernel(tc, x, mfs, rules, out):
             out=rcodes[:].bitcast(FP8X4), scales=rscales[:], in_=rg[:].rearrange("p o t -> p (o t)")
         )
         for u in range(NU):
-            nbs[u] = nbp.tile(
-                [P, QUAD if u == NU - 1 else 2 * UNITS[u], 4 * P], BF16, tag="nb", name="nb", align_bytes=64
-            )
+            nbs[u] = nbp.tile([P, products(u), 4 * P], BF16, tag="nb", name="nb", align_bytes=64)
             k = [k for k in range(len(SUBS)) if sub_start[k] <= first[u]][-1]
             if first[u] == sub_start[k] and k + 1 < len(SUBS):
                 lo, pr, more = tables_of(k + 1)
-                order = pr[:5] + lo[:3] + pr[5:8] + lo[3:] + pr[8:9] + more + pr[9:]
-                pending = pending + [(f, WIDE if f in (pr[4], pr[8], pr[9], lo[5]) else 1) for f in order]
-            if u == 3:
-                last_tables, xt, yt = product_tables(
+                order = pr[:5] + lo[:3] + pr[5:] + lo[3:] + more
+                pending = pending + [(f, WIDE if f in (pr[4], lo[5]) else 1) for f in order]
+            if first[u] == sub_start[-1]:
+                last_tables, factors = product_tables(
                     "z", QUAD, lambda i: mb[:, i, :, NJ - QUAD : NJ].rearrange("p m j -> p j m"), t1[:, NJ - QUAD : NJ]
                 )
-                prod[NQ - 1] = (xt, yt, 0)
-            left = [v for v in range(u, NU) if k + 1 == len(SUBS) or first[v] < sub_start[k + 1]]
-            share = sum(w for f, w in pending) / len(left)
+                prod[NU - 1] = [(factors, 0, 0, QUAD)]
+                pending = pending + [(f, 1) for f in last_tables]
+            left = [v for v in range(u, NU) if v < NU - 1 and (k + 1 == len(SUBS) or first[v] < sub_start[k + 1])]
+            share = sum(w for f, w in pending) / max(1, len(left))
             n_now, sum_now = 0, 0
             for f, w in pending:
                 if sum_now < share:
                     n_now, sum_now = n_now + 1, sum_now + w
             extras, pending = [f for f, w in pending[:n_now]], pending[n_now:]
             if u == 3:
-                extras = extras + last_tables
-            work = [direct(u), direct(u, 1) if u == NU - 1 else log_sum(u)]
+                odd_tables, factors = product_tables("o", 8, odd, t1[:].rearrange("p (n w) -> p w n", w=16)[:, 13, :])
+                for v in extra:
+                    prod.setdefault(v, []).append((factors, first[v] // 4, 2 * UNITS[v], 2 * UNITS[v] + 1))
+                extras = odd_tables + extras
+            work = seven(u) + ([] if u == NU - 1 else log_sum(u))
+            work += [block(u, slot, c) for slot in range(products(u)) for c in range(4)]
             if u >= 2:
                 work.append(lambda: quantise(u - 2))
+            if u >= 4:
+                for q in range(first[u - 4], first[u - 4] + UNITS[u - 4]):
+                    if q in on_vector:
+                        work.insert(1, lambda q=q: put_out(q, nc.vector.tensor_copy))
             done = 0
             for i, f in enumerate(work):
                 f()
@@ -399,7 +444,8 @@ def tile_extendedanfis_t_kernel(tc, x, mfs, rules, out):
                 multiply_unit(u - 3)
             if u >= 4:
                 for q in range(UNITS[u - 4]):
-                    put_out(first[u - 4] + q, nc.scalar.copy)
+                    if first[u - 4] + q not in on_vector:
+                        put_out(first[u - 4] + q, nc.scalar.copy)
             if u >= 1:
                 for c in range(words(u - 1)):
                     evacuate_words(u - 1, c, nc.scalar.copy)

@@ -25,7 +25,8 @@ SUBS = [16, 24, 32, 56]
 ON_VECTOR = 3
 EXTRA = 2
 WIDE = 4
-GROUP = 4
+GROUP = 2
+ALONE = 6
 
 
 def tile_extendedanfis_t_kernel(tc, x, mfs, rules, out):
@@ -38,7 +39,7 @@ def tile_extendedanfis_t_kernel(tc, x, mfs, rules, out):
         nbp = ctx.enter_context(tc.tile_pool(name="nbp", bufs=4))
         grp = ctx.enter_context(tc.tile_pool(name="grp", bufs=4))
         cdp = ctx.enter_context(tc.tile_pool(name="cdp", bufs=4))
-        osp = ctx.enter_context(tc.tile_pool(name="osp", bufs=3))
+        osp = ctx.enter_context(tc.tile_pool(name="osp", bufs=5))
         tps = ctx.enter_context(tc.psum_pool(name="tps", bufs=6))
         ops = ctx.enter_context(tc.psum_pool(name="ops", bufs=2))
         ctx.enter_context(tc.manual_schedule())
@@ -196,7 +197,7 @@ def tile_extendedanfis_t_kernel(tc, x, mfs, rules, out):
         prod, logs = {}, {}
         on_vector = range(sum(SUBS[:-1]) // QUAD, NQ, 4)
         first = [sum(UNITS[:u]) for u in range(NU)]
-        extra = [u for u in range(4, NU) if first[u] % 4 == 2 and UNITS[u] == 2]
+        extra = [u for u in range(5, NU) if first[u] % 4 == 2 and UNITS[u] == 2]
 
         def products(u):
             return QUAD if u == NU - 1 else 2 * UNITS[u] + (u in extra)
@@ -330,7 +331,10 @@ def tile_extendedanfis_t_kernel(tc, x, mfs, rules, out):
 
         def multiply(u, q, slots, c=0):
             codes, scales = cds[u, c]
-            po = ops.tile([P, QUAD, O], F32, tag="po", name="po")
+            if u < NU - 3:
+                po = ops.tile([P, QUAD, O], F32, tag="po", name="po")
+            else:
+                po = tps.tile([P, QUAD, O], F32, tag="tp", name="tp")
             pos[first[u] + q, c] = po
             for jj, slot in enumerate(slots):
                 nc.tensor.matmul_mx(
@@ -360,7 +364,7 @@ def tile_extendedanfis_t_kernel(tc, x, mfs, rules, out):
                 out=rows.rearrange("p (w c) o -> p c w o", c=2),
                 in_=pos[sq, 0][:].rearrange("p (c w) o -> p c w o", c=2),
             )
-            if grp_i == NQ // GROUP - 1:
+            if sq >= NQ - ALONE:
                 store(sq * QUAD, (sq + 1) * QUAD, rows)
             elif pos_i == GROUP - 1:
                 store(grp_i * GROUP * QUAD, (grp_i + 1) * GROUP * QUAD, ost[:])
@@ -382,22 +386,22 @@ def tile_extendedanfis_t_kernel(tc, x, mfs, rules, out):
         lo, pr, more = tables_of(0)
         pending = [(f, 1) for f in more]
         nc.vector.tensor_copy(out=rg[:], in_=rl[:].rearrange("p t o -> p o t"))
-        head = lo + [sum_pair(0, 4)] + pr[:1] + four(0)[:1] + pr[1:2] + four(0)[1:]
-        head += [sum_pair(4, 8)] + pr[2:3] + four(1)[:1] + [sum_pair(8, I)] + four(1)[1:] + pr[3:4]
+        h0, c23, c45, c68, yt, reciprocal, h, at = pr
+        fa, fb = four(0), four(1)
+        head = lo + [sum_pair(0, 4), c23, fa[0]] + log_sum(0) + [fa[1], h0]
+        head += [sum_pair(4, 8), c45, fb[0], at, sum_pair(8, I), c68, fb[1], yt]
+        head += [tt(t1[:], t2[:, 0, :], sums[:, 8, :], ALU.mult)] + seven(0)
         head += [
-            tt(t1[:], t2[:, 0, :], sums[:, 8, :], ALU.mult),
-            pr[4],
             tt(t1[:], t1[:], t2[:, 1, :], ALU.mult),
             lambda: nc.vector.tensor_scalar_add(out=t1[:], in0=t1[:], scalar1=EPS),
+            reciprocal,
+            h,
         ]
-        for f in head + pr[5:]:
+        for f in head:
             f()
         nc.scalar.activation(out=lns[:], in_=t1[:], func=ACT.Ln)
         nc.scalar.activation(out=warm[:], in_=lns[:, 0:1], func=ACT.Exp, scale=-0.5)
 
-        nc.vector.quantize_mx(
-            out=rcodes[:].bitcast(FP8X4), scales=rscales[:], in_=rg[:].rearrange("p o t -> p (o t)")
-        )
         for u in range(NU):
             nbs[u] = nbp.tile([P, products(u), 4 * P], BF16, tag="nb", name="nb", align_bytes=64)
             k = [k for k in range(len(SUBS)) if sub_start[k] <= first[u]][-1]
@@ -405,6 +409,11 @@ def tile_extendedanfis_t_kernel(tc, x, mfs, rules, out):
                 lo, pr, more = tables_of(k + 1)
                 order = pr[:5] + lo[:3] + pr[5:] + lo[3:] + more
                 pending = pending + [(f, WIDE if f in (pr[4], lo[5]) else 1) for f in order]
+            if first[u] == sub_start[1]:
+                odd_tables, factors = product_tables("o", 8, odd, t1[:].rearrange("p (n w) -> p w n", w=16)[:, 13, :])
+                for v in extra:
+                    prod.setdefault(v, []).append((factors, first[v] // 4, 2 * UNITS[v], 2 * UNITS[v] + 1))
+                pending = [(f, 1) for f in odd_tables] + pending
             if first[u] == sub_start[-1]:
                 last_tables, factors = product_tables(
                     "z", QUAD, lambda i: mb[:, i, :, NJ - QUAD : NJ].rearrange("p m j -> p j m"), t1[:, NJ - QUAD : NJ]
@@ -418,12 +427,7 @@ def tile_extendedanfis_t_kernel(tc, x, mfs, rules, out):
                 if sum_now < share:
                     n_now, sum_now = n_now + 1, sum_now + w
             extras, pending = [f for f, w in pending[:n_now]], pending[n_now:]
-            if u == 3:
-                odd_tables, factors = product_tables("o", 8, odd, t1[:].rearrange("p (n w) -> p w n", w=16)[:, 13, :])
-                for v in extra:
-                    prod.setdefault(v, []).append((factors, first[v] // 4, 2 * UNITS[v], 2 * UNITS[v] + 1))
-                extras = odd_tables + extras
-            work = seven(u) + ([] if u == NU - 1 else log_sum(u))
+            work = [] if u == 0 else seven(u) + ([] if u == NU - 1 else log_sum(u))
             work += [block(u, slot, c) for slot in range(products(u)) for c in range(4)]
             if u >= 2:
                 work.append(lambda: quantise(u - 2))
@@ -438,6 +442,10 @@ def tile_extendedanfis_t_kernel(tc, x, mfs, rules, out):
                 for e in extras[done:want]:
                     e()
                 done = want
+            if u == 0:
+                nc.vector.quantize_mx(
+                    out=rcodes[:].bitcast(FP8X4), scales=rscales[:], in_=rg[:].rearrange("p o t -> p (o t)")
+                )
             if u >= 1:
                 transposes(u - 1)
             if u >= 3:
@@ -452,19 +460,19 @@ def tile_extendedanfis_t_kernel(tc, x, mfs, rules, out):
                 evacuate_logs(u - 1)
 
         transposes(NU - 1)
-        put_out(NQ - 6, nc.vector.tensor_copy)
-        put_out(NQ - 5, nc.vector.tensor_copy)
-        multiply_unit(NU - 3)
-        quantise(NU - 2)
         evacuate_words(NU - 1, 0, nc.vector.tensor_copy)
         evacuate_words(NU - 1, 1, nc.scalar.copy)
-        quantise(NU - 1, 0, 2)
-        quantise(NU - 1, 1, 2)
-        put_out(NQ - 4, nc.scalar.copy)
+        put_out(NQ - 6, nc.vector.tensor_copy)
+        put_out(NQ - 5, nc.scalar.copy)
+        multiply_unit(NU - 3)
+        quantise(NU - 2)
         multiply_unit(NU - 2)
-        put_out(NQ - 3, nc.vector.tensor_copy)
+        quantise(NU - 1, 0, 2)
         multiply(NU - 1, 0, [0, 1], 0)
-        put_out(NQ - 2, nc.scalar.copy)
+        quantise(NU - 1, 1, 2)
         multiply(NU - 1, 0, [0, 1], 1)
+        put_out(NQ - 4, nc.scalar.copy)
+        put_out(NQ - 3, nc.vector.tensor_copy)
+        put_out(NQ - 2, nc.scalar.copy)
         put_out_last(0, nc.vector.tensor_copy)
         put_out_last(1, nc.scalar.copy)

from contextlib import ExitStack

import concourse.mybir as mybir
from concourse.masks import make_identity

F32 = mybir.dt.float32
BF16 = mybir.dt.bfloat16
U32 = mybir.dt.uint32
U8 = mybir.dt.uint8
FP8X4 = mybir.dt.float8_e4m3fn_x4
ALU = mybir.AluOpType
ACT = mybir.ActivationFunctionType

P = 128
B, I, M, O = 16384, 9, 2, 128
R = 512
NJ = B // P
EPS = 1e-6
FLOPS = 2 * B * R * O
QUAD = 4
NQ = NJ // QUAD
UNITS = [1, 1] + [2] * 14 + [1, 1]
NU = len(UNITS)
SUBS = [16, 24, 32, 56]
ON_VECTOR = 3
EXTRA = 2
WIDE = 4
GROUP = 2
ALONE = 6


def tile_extendedanfis_t_kernel(tc, x, mfs, rules, out):
    nc = tc.nc
    with ExitStack() as ctx:
        const = ctx.enter_context(tc.tile_pool(name="const", bufs=1))
        small = ctx.enter_context(tc.tile_pool(name="small", bufs=2))
        l7p = ctx.enter_context(tc.tile_pool(name="l7p", bufs=3))
        s7p = ctx.enter_context(tc.tile_pool(name="s7p", bufs=2))
        nbp = ctx.enter_context(tc.tile_pool(name="nbp", bufs=4))
        grp = ctx.enter_context(tc.tile_pool(name="grp", bufs=4))
        cdp = ctx.enter_context(tc.tile_pool(name="cdp", bufs=4))
        osp = ctx.enter_context(tc.tile_pool(name="osp", bufs=5))
        tps = ctx.enter_context(tc.psum_pool(name="tps", bufs=6))
        ops = ctx.enter_context(tc.psum_pool(name="ops", bufs=2))
        ctx.enter_context(tc.manual_schedule())

        ones = const.tile([P, 1], F32)
        nc.vector.memset(ones[:], 1.0)
        warm = const.tile([P, 1], F32)
        nc.scalar.activation(out=warm[:], in_=ones[:], func=ACT.Exp)

        mf = const.tile([P, I * M * 2], BF16)
        nc.sync.dma_start(out=mf[:], in_=mfs.rearrange("i m c -> (i m c)").partition_broadcast(P))
        xs = const.tile([P, NJ * I], BF16)
        nc.sync.dma_start(out=xs[:], in_=x.rearrange("(p j) i -> p (j i)", j=NJ))
        rl = const.tile([P, 4, O], BF16)
        nc.sync.dma_start(out=rl[:], in_=rules.rearrange("(p t) o -> p t o", t=4))

        ident = const.tile([P, P], F32)
        make_identity(nc, ident[:])

        mfv = mf[:].rearrange("p (k c) -> p k c", c=2)
        sg = const.tile([P, I * M], F32)
        nc.vector.scalar_tensor_tensor(
            out=sg[:], in0=mfv[:, :, 1], scalar=-1.0, in1=mfv[:, :, 1], op0=ALU.mult, op1=ALU.max
        )
        nc.vector.tensor_scalar_add(out=sg[:], in0=sg[:], scalar1=EPS)
        rs = const.tile([P, I * M], F32)
        nc.vector.reciprocal(out=rs[:], in_=sg[:])
        bs = const.tile([P, I * M], F32)
        nc.vector.scalar_tensor_tensor(
            out=bs[:], in0=mfv[:, :, 0], scalar=-1.0, in1=rs[:], op0=ALU.mult, op1=ALU.mult
        )

        rg = const.tile([P, O, 4], BF16, align_bytes=64)
        rcodes = const.tile([P, O], U32, align_bytes=64)
        rscales = const.tile([P, O], U8, align_bytes=64)

        out_v = out.rearrange("(p j) o -> p j o", j=NJ)

        def tt(o, i0, i1, op):
            return lambda: nc.vector.tensor_tensor(out=o, in0=i0, in1=i1, op=op)

        def outer(o, u, v, op=ALU.mult):
            n, nu = u.shape[1], u.shape[2]
            nv = v.shape[2]
            return tt(
                o,
                u.unsqueeze(3).to_broadcast([P, n, nu, nv]),
                v.unsqueeze(2).to_broadcast([P, n, nu, nv]),
                op,
            )

        def flat(t):
            return t[:].rearrange("p j a b -> p j (a b)")

        z = const.tile([P, I, M, NJ], F32)
        mb = const.tile([P, I, M, NJ], F32)
        sums = const.tile([P, I, NJ], F32)
        t4 = const.tile([P, 2, 2, NJ], F32)
        t2 = const.tile([P, 2, NJ], F32)
        t1 = const.tile([P, NJ], F32)
        lns = const.tile([P, NJ], F32)
        xv = xs[:].rearrange("p (j i) -> p i j", i=I)

        def squares(i0, i1):
            for i in range(i0, i1):
                for m in range(M):
                    k = i * M + m
                    nc.scalar.activation(
                        out=z[:, i, m, :],
                        in_=xv[:, i, :],
                        func=ACT.Square,
                        scale=rs[:, k : k + 1],
                        bias=bs[:, k : k + 1],
                    )

        def exponentials(i0, i1):
            nc.scalar.activation(
                out=mb[:, i0:i1, :, :].rearrange("p i m j -> p (i m j)"),
                in_=z[:, i0:i1, :, :].rearrange("p i m j -> p (i m j)"),
                func=ACT.Exp,
                scale=-0.5,
            )

        zv = const.tile([P, ON_VECTOR, M, NJ], F32)
        for i in range(I - ON_VECTOR, I):
            for m in range(M):
                k = i * M + m
                nc.vector.tensor_scalar(
                    out=zv[:, i - (I - ON_VECTOR), m, :],
                    in0=xv[:, i, :],
                    scalar1=rs[:, k : k + 1],
                    scalar2=bs[:, k : k + 1],
                    op0=ALU.mult,
                    op1=ALU.add,
                )
        nc.vector.tensor_tensor(out=z[:, I - ON_VECTOR : I, :, :], in0=zv[:], in1=zv[:], op=ALU.mult)
        squares(0, I - ON_VECTOR)
        exponentials(0, 4)
        exponentials(4, 8)
        exponentials(8, I)

        def product_tables(pre, n, mem, den):
            rinv = small.tile([P, n], F32, tag=pre + "rinv", name=pre + "rinv")
            h0 = small.tile([P, n, 2, 2], F32, tag=pre + "h0", name=pre + "h0")
            h = small.tile([P, n, 4], F32, tag=pre + "h", name=pre + "h")
            c23 = small.tile([P, n, 2, 2], F32, tag=pre + "c23", name=pre + "c23")
            c45 = small.tile([P, n, 2, 2], F32, tag=pre + "c45", name=pre + "c45")
            c68 = small.tile([P, n, 2, 2], F32, tag=pre + "c68", name=pre + "c68")
            at = small.tile([P, n, 2, 4], F32, tag=pre + "at", name=pre + "at")
            yt = small.tile([P, n, 4, 4], F32, tag=pre + "yt", name=pre + "yt")
            ops_ = [
                outer(h0[:], mem(0), mem(1)),
                outer(c23[:], mem(2), mem(3)),
                outer(c45[:], mem(4), mem(5)),
                outer(c68[:], mem(6), mem(8)),
                outer(yt[:], flat(c45), flat(c68)),
                lambda: nc.vector.reciprocal(out=rinv[:], in_=den),
                tt(h[:], flat(h0), rinv[:].unsqueeze(2).to_broadcast([P, n, 4]), ALU.mult),
                outer(at[:], mem(7), flat(c23)),
            ]
            return ops_, (flat(at), flat(yt), h)

        def log_tables(pre, n, sq, lns_):
            l01 = small.tile([P, n, 2, 2], F32, tag=pre + "l01", name=pre + "l01")
            la = small.tile([P, n, 4, 2], F32, tag=pre + "la", name=pre + "la")
            l34 = small.tile([P, n, 2, 2], F32, tag=pre + "l34", name=pre + "l34")
            l56 = small.tile([P, n, 2, 2], F32, tag=pre + "l56", name=pre + "l56")
            lb = small.tile([P, n, 4, 4], F32, tag=pre + "lb", name=pre + "lb")
            l78 = small.tile([P, n, 2, 2], F32, tag=pre + "l78", name=pre + "l78")
            lt = small.tile([P, n, 4], F32, tag=pre + "lt", name=pre + "lt")
            ops_ = [
                outer(l01[:], sq(0), sq(1), ALU.add),
                outer(l34[:], sq(3), sq(4), ALU.add),
                outer(l56[:], sq(5), sq(6), ALU.add),
                outer(la[:], flat(l01), sq(2), ALU.add),
                outer(l78[:], sq(7), sq(8), ALU.add),
                outer(lb[:], flat(l34), flat(l56), ALU.add),
            ]
            last = [
                lambda: nc.vector.scalar_tensor_tensor(
                    out=lt[:],
                    in0=lns_.unsqueeze(2).to_broadcast([P, n, 4]),
                    scalar=2.0,
                    in1=flat(l78),
                    op0=ALU.mult,
                    op1=ALU.add,
                )
            ]
            return ops_, last, flat(la), flat(lb), lt

        def pick(t, i, j0, n, c):
            return t[:, i, :, j0 : j0 + 2 * n].rearrange("p m (n c) -> p c n m", c=2)[:, c, :, :]

        s7s, nbs, l7s, gs, cds, pos, osts, tpl = {}, {}, {}, {}, {}, {}, {}, {}
        prod, logs = {}, {}
        on_vector = range(sum(SUBS[:-1]) // QUAD, NQ, 4)
        first = [sum(UNITS[:u]) for u in range(NU)]
        extra = [u for u in range(5, NU) if first[u] % 4 == 2 and UNITS[u] == 2]

        def products(u):
            return QUAD if u == NU - 1 else 2 * UNITS[u] + (u in extra)

        sub_start = [sum(SUBS[:k]) // QUAD for k in range(len(SUBS))]

        def odd(i):
            return mb[:, i, :, :].rearrange("p m (n w) -> p w n m", w=16)[:, 13, :, :]

        def tables_of(k):
            j0, n = QUAD * sub_start[k], SUBS[k] // 2
            pr, factors = product_tables(
                "a", n, lambda i: pick(mb, i, j0, n, 0), t1[:, j0 : j0 + 2 * n].rearrange("p (n c) -> p c n", c=2)[:, 0, :]
            )
            lo, last, la, lb, lt = log_tables(
                "b", n, lambda i: pick(z, i, j0, n, 1), lns[:, j0 : j0 + 2 * n].rearrange("p (n c) -> p c n", c=2)[:, 1, :]
            )
            for u in range(NU - 1):
                q = first[u] - sub_start[k]
                if 0 <= q < SUBS[k] // QUAD:
                    prod.setdefault(u, []).append((factors, 2 * q, 0, 2 * UNITS[u]))
                    logs[first[u]] = (la, lb, lt, 2 * q)
            return lo, pr, last

        def seven(u):
            s7s[u] = s7p.tile([P, products(u), 2, 64], F32, tag="s7", name="s7")
            ops_ = []
            for (at, yt, h), n, s0, s1 in prod[u]:
                ops_.append(
                    outer(
                        s7s[u][:, s0:s1, :, :].rearrange("p k e (a b) -> p k (e a) b", b=16),
                        at[:, n : n + s1 - s0, :],
                        yt[:, n : n + s1 - s0, :],
                    )
                )
            return ops_

        def block(u, slot, c):
            (at, yt, h), n, s0, s1 = [e for e in prod[u] if e[2] <= slot < e[3]][0]
            n -= s0
            return lambda: nc.vector.tensor_scalar(
                out=nbs[u][:, slot, :].rearrange("p (e w) -> p e w", e=2)[:, :, 64 * c : 64 * c + 64],
                in0=s7s[u][:, slot, :, :],
                scalar1=h[:, n + slot, c : c + 1],
                scalar2=None,
                op0=ALU.mult,
            )

        def log_sum(u):
            la, lb, lt, n = logs[first[u]]
            l7s[u] = l7p.tile([P, 2 * UNITS[u], P], F32, tag="l7", name="l7")
            runs = [(0, EXTRA), (EXTRA + 1, 2 * UNITS[u])] if u in extra else [(0, 2 * UNITS[u])]
            return [
                outer(
                    l7s[u][:, k0:k1, :].rearrange("p k (a b) -> p k a b", b=16),
                    la[:, n + k0 : n + k1, :],
                    lb[:, n + k0 : n + k1, :],
                    ALU.add,
                )
                for k0, k1 in runs
            ]

        def quantise(u, c=0, parts=1):
            w = QUAD * UNITS[u] * P // parts
            codes = cdp.tile([P, w], U32, tag="codes", name="codes", align_bytes=64)
            scales = cdp.tile([P, w], U8, tag="scales", name="scales", align_bytes=64)
            cds[u, c] = (codes, scales)
            nc.vector.quantize_mx(
                out=codes[:].bitcast(FP8X4), scales=scales[:], in_=gs[u][:].rearrange("p k b t -> p (k b t)")[:, 4 * w * c : 4 * w * (c + 1)]
            )

        def words(u):
            return 2 if u == NU - 1 else UNITS[u]

        def by_logs(u):
            return [k for k in range(2 * UNITS[u]) if not (u in extra and k == EXTRA)]

        def transposes(u):
            for c in range(words(u)):
                tp = tps.tile([P, 4, P], F32, tag="tp", name="tp")
                tpl[u, c] = tp
                for k in range(2):
                    for h in range(2):
                        pairs = nbs[u][:, 2 * c + k, 2 * P * h : 2 * P * (h + 1)].bitcast(F32)
                        nc.tensor.transpose(tp[:, 2 * k + h, :], pairs, ident[:])
            if u == NU - 1:
                return
            if u in extra:
                tp = tps.tile([P, 4, P], F32, tag="tp", name="tp")
                tpl[u, words(u) + EXTRA] = tp
                for h in range(2):
                    pairs = nbs[u][:, 2 * UNITS[u], 2 * P * h : 2 * P * (h + 1)].bitcast(F32)
                    nc.tensor.transpose(tp[:, h, :], pairs, ident[:])
            la, lb, lt, n = logs[first[u]]
            for k in by_logs(u):
                tp = tps.tile([P, 4, P], F32, tag="tp", name="tp")
                tpl[u, words(u) + k] = tp
                for t in range(4):
                    nc.tensor.matmul(tp[:, t, :], l7s[u][:, k, :], ident[:], start=True, stop=False, is_transpose=True)
                    nc.tensor.matmul(
                        tp[:, t, :],
                        lt[:, n + k, t : t + 1].to_broadcast([P, P]),
                        ident[:],
                        start=False,
                        stop=True,
                        is_transpose=True,
                    )

        def evacuate_words(u, c, copy):
            if c == 0:
                gs[u] = grp.tile([P, QUAD * UNITS[u], P, 4], BF16, tag="g", name="g", align_bytes=64)
            copy(
                out=gs[u][:, 2 * c : 2 * c + 2, :, :].bitcast(F32),
                in_=tpl[u, c][:].rearrange("p (k h) b -> p k b h", h=2),
            )

        def evacuate_logs(u):
            if u in extra:
                slot = 2 * UNITS[u] + EXTRA
                nc.scalar.copy(
                    out=gs[u][:, slot, :, :].bitcast(F32),
                    in_=tpl[u, words(u) + EXTRA][:, 0:2, :].rearrange("p h b -> p b h"),
                )
            for k in by_logs(u):
                nc.scalar.activation(
                    out=gs[u][:, 2 * UNITS[u] + k, :, :],
                    in_=tpl[u, words(u) + k][:].rearrange("p t b -> p b t"),
                    func=ACT.Exp,
                    scale=-0.5,
                )

        def multiply(u, q, slots, c=0):
            codes, scales = cds[u, c]
            if u < NU - 3:
                po = ops.tile([P, QUAD, O], F32, tag="po", name="po")
            else:
                po = tps.tile([P, QUAD, O], F32, tag="tp", name="tp")
            pos[first[u] + q, c] = po
            for jj, slot in enumerate(slots):
                nc.tensor.matmul_mx(
                    out=po[:, jj, :],
                    lhsT=codes[:, slot * P : (slot + 1) * P].bitcast(FP8X4),
                    lhsT_scale=scales[:, slot * P : (slot + 1) * P],
                    rhs=rcodes[:].bitcast(FP8X4),
                    rhs_scale=rscales[:],
                    start=True,
                    stop=True,
                )

        def multiply_unit(u):
            for q in range(UNITS[u]):
                multiply(u, q, [2 * q, 2 * q + 1, 2 * (UNITS[u] + q), 2 * (UNITS[u] + q) + 1])

        def store(j0, j1, rows):
            nc.sync.dma_start(out=out_v[:, j0:j1, :], in_=rows)

        def put_out(sq, copy):
            grp_i, pos_i = sq // GROUP, sq % GROUP
            if pos_i == 0:
                osts[grp_i] = osp.tile([P, GROUP * QUAD, O], F32, tag="ost", name="ost")
            ost = osts[grp_i]
            rows = ost[:, pos_i * QUAD : (pos_i + 1) * QUAD, :]
            copy(
                out=rows.rearrange("p (w c) o -> p c w o", c=2),
                in_=pos[sq, 0][:].rearrange("p (c w) o -> p c w o", c=2),
            )
            if sq >= NQ - ALONE:
                store(sq * QUAD, (sq + 1) * QUAD, rows)
            elif pos_i == GROUP - 1:
                store(grp_i * GROUP * QUAD, (grp_i + 1) * GROUP * QUAD, ost[:])

        def put_out_last(c, copy):
            rows = osts[NQ // GROUP - 1][:, (GROUP - 1) * QUAD + 2 * c : (GROUP - 1) * QUAD + 2 * c + 2, :]
            copy(out=rows, in_=pos[NQ - 1, c][:, 0:2, :])
            store(NJ - QUAD + 2 * c, NJ - QUAD + 2 * c + 2, rows)

        def sum_pair(i0, i1):
            return tt(sums[:, i0:i1, :], mb[:, i0:i1, 0, :], mb[:, i0:i1, 1, :], ALU.add)

        def four(c):
            return [
                tt(t4[:, c, :, :], sums[:, 4 * c : 4 * c + 2, :], sums[:, 4 * c + 2 : 4 * c + 4, :], ALU.mult),
                tt(t2[:, c, :], t4[:, c, 0, :], t4[:, c, 1, :], ALU.mult),
            ]

        lo, pr, more = tables_of(0)
        pending = [(f, 1) for f in more]
        nc.vector.tensor_copy(out=rg[:], in_=rl[:].rearrange("p t o -> p o t"))
        h0, c23, c45, c68, yt, reciprocal, h, at = pr
        fa, fb = four(0), four(1)
        head = lo + [sum_pair(0, 4), c23, fa[0]] + log_sum(0) + [fa[1], h0]
        head += [sum_pair(4, 8), c45, fb[0], at, sum_pair(8, I), c68, fb[1], yt]
        head += [tt(t1[:], t2[:, 0, :], sums[:, 8, :], ALU.mult)] + seven(0)
        head += [
            tt(t1[:], t1[:], t2[:, 1, :], ALU.mult),
            lambda: nc.vector.tensor_scalar_add(out=t1[:], in0=t1[:], scalar1=EPS),
            reciprocal,
            h,
        ]
        for f in head:
            f()
        nc.scalar.activation(out=lns[:], in_=t1[:], func=ACT.Ln)
        nc.scalar.activation(out=warm[:], in_=lns[:, 0:1], func=ACT.Exp, scale=-0.5)

        for u in range(NU):
            nbs[u] = nbp.tile([P, products(u), 4 * P], BF16, tag="nb", name="nb", align_bytes=64)
            k = [k for k in range(len(SUBS)) if sub_start[k] <= first[u]][-1]
            if first[u] == sub_start[k] and k + 1 < len(SUBS):
                lo, pr, more = tables_of(k + 1)
                order = pr[:5] + lo[:3] + pr[5:] + lo[3:] + more
                pending = pending + [(f, WIDE if f in (pr[4], lo[5]) else 1) for f in order]
            if first[u] == sub_start[1]:
                odd_tables, factors = product_tables("o", 8, odd, t1[:].rearrange("p (n w) -> p w n", w=16)[:, 13, :])
                for v in extra:
                    prod.setdefault(v, []).append((factors, first[v] // 4, 2 * UNITS[v], 2 * UNITS[v] + 1))
                pending = [(f, 1) for f in odd_tables] + pending
            if first[u] == sub_start[-1]:
                last_tables, factors = product_tables(
                    "z", QUAD, lambda i: mb[:, i, :, NJ - QUAD : NJ].rearrange("p m j -> p j m"), t1[:, NJ - QUAD : NJ]
                )
                prod[NU - 1] = [(factors, 0, 0, QUAD)]
                pending = pending + [(f, 1) for f in last_tables]
            left = [v for v in range(u, NU) if v < NU - 1 and (k + 1 == len(SUBS) or first[v] < sub_start[k + 1])]
            share = sum(w for f, w in pending) / max(1, len(left))
            n_now, sum_now = 0, 0
            for f, w in pending:
                if sum_now < share:
                    n_now, sum_now = n_now + 1, sum_now + w
            extras, pending = [f for f, w in pending[:n_now]], pending[n_now:]
            work = [] if u == 0 else seven(u) + ([] if u == NU - 1 else log_sum(u))
            work += [block(u, slot, c) for slot in range(products(u)) for c in range(4)]
            if u >= 2:
                work.append(lambda: quantise(u - 2))
            if u >= 4:
                for q in range(first[u - 4], first[u - 4] + UNITS[u - 4]):
                    if q in on_vector:
                        work.insert(1, lambda q=q: put_out(q, nc.vector.tensor_copy))
            done = 0
            for i, f in enumerate(work):
                f()
                want = (i + 1) * len(extras) // len(work)
                for e in extras[done:want]:
                    e()
                done = want
            if u == 0:
                nc.vector.quantize_mx(
                    out=rcodes[:].bitcast(FP8X4), scales=rscales[:], in_=rg[:].rearrange("p o t -> p (o t)")
                )
            if u >= 1:
                transposes(u - 1)
            if u >= 3:
                multiply_unit(u - 3)
            if u >= 4:
                for q in range(UNITS[u - 4]):
                    if first[u - 4] + q not in on_vector:
                        put_out(first[u - 4] + q, nc.scalar.copy)
            if u >= 1:
                for c in range(words(u - 1)):
                    evacuate_words(u - 1, c, nc.scalar.copy)
                evacuate_logs(u - 1)

        transposes(NU - 1)
        evacuate_words(NU - 1, 0, nc.vector.tensor_copy)
        evacuate_words(NU - 1, 1, nc.scalar.copy)
        put_out(NQ - 6, nc.vector.tensor_copy)
        put_out(NQ - 5, nc.scalar.copy)
        multiply_unit(NU - 3)
        quantise(NU - 2)
        multiply_unit(NU - 2)
        quantise(NU - 1, 0, 2)
        multiply(NU - 1, 0, [0, 1], 0)
        quantise(NU - 1, 1, 2)
        multiply(NU - 1, 0, [0, 1], 1)
        put_out(NQ - 4, nc.scalar.copy)
        put_out(NQ - 3, nc.vector.tensor_copy)
        put_out(NQ - 2, nc.scalar.copy)
        put_out_last(0, nc.vector.tensor_copy)
        put_out_last(1, nc.scalar.copy)
